import numpy as np
import ml_dtypes


def mxq(x, axis, fmt="e4m3"):
    dtype, down = {"e4m3": (ml_dtypes.float8_e4m3fn, 7), "e5m2": (ml_dtypes.float8_e5m2, 14)}[fmt]
    v = np.moveaxis(np.asarray(x, np.float32).astype(ml_dtypes.bfloat16).astype(np.float64), axis, -1)
    blocks = v.reshape(v.shape[:-1] + (-1, 32))
    amax = np.abs(blocks).max(-1, keepdims=True)
    byte = np.maximum(np.where(amax > 0, np.frexp(amax)[1] - 1 + 127, 0) - down, 1)
    scale = np.exp2(byte - 127.0)
    codes = (blocks / scale).astype(np.float32).astype(dtype).astype(np.float64)
    return np.moveaxis((codes * scale).reshape(v.shape), -1, axis)


WIDE = False


def mx_kscale(k):
    if not WIDE:
        return np.ones(k)
    levels = np.array([10, -10, 5, -5, 0])
    a = np.random.permutation(np.resize(levels, k // 512 * 4)).reshape(k // 512, 4)
    idx = np.arange(k)
    return np.exp2(a[idx // 512, idx % 128 // 32])


BF16 = ml_dtypes.bfloat16


def bf(x):
    return np.asarray(x, np.float32).astype(BF16)


def f64(x):
    return np.asarray(x).astype(np.float64)


B, SY, SX, D, F = 2, 2048, 2048, 512, 1024
EPS = 1e-5


def layer_norm_all(t):
    mu = t.mean()
    var = np.square(t - mu).mean()
    return (t - mu) / np.sqrt(var + EPS)


def setup_inputs():
    t = mx_kscale(F)
    return {"h2": bf(np.random.standard_normal((B, SY, D))),
            "w_ff1": bf(np.random.standard_normal((F, D)) / np.sqrt(D) * t[:, None]),
            "b_ff1": bf(np.random.standard_normal(F) * 0.3 * t),
            "w_ff2": bf(np.random.standard_normal((D, F)) * 1.4 / np.sqrt(F) / t[None, :]),
            "b_ff2": bf(0.2 + 0.2 * np.random.standard_normal(D))}


def reference(h2, w_ff1, b_ff1, w_ff2, b_ff2):
    h = f64(h2)
    a = np.maximum((mxq(h, 2, "e4m3") @ mxq(f64(w_ff1), 1, "e4m3").T) + f64(b_ff1), 0.0)
    ff = (mxq(a, 2, "e4m3") @ mxq(f64(w_ff2), 1, "e4m3").T) + f64(b_ff2)
    return layer_norm_all(h + ff)

@@ -1,0 +1,300 @@
+from contextlib import ExitStack
+
+import concourse.mybir as mybir
+from concourse.masks import make_identity
+
+F32 = mybir.dt.float32
+BF16 = mybir.dt.bfloat16
+U32 = mybir.dt.uint32
+U8 = mybir.dt.uint8
+FP8X4 = mybir.dt.float8_e4m3fn_x4
+ACT = mybir.ActivationFunctionType
+ALU = mybir.AluOpType
+
+P = 128
+PACK = 4
+D = 512
+F = 1024
+TOKENS = 2 * 2048
+BLOCK = 512
+SUB = BLOCK // P
+N_BLOCKS = TOKENS // BLOCK
+F_TILES = F // P
+D_TILES = D // P
+F_PASSES = F // (P * PACK)
+EPS = 1e-5
+
+FLOPS = 2 * TOKENS * D * F * 2
+
+
+def tile_decoderblock_pb_t_kernel(tc, h2, w_ff1, b_ff1, w_ff2, b_ff2, out):
+    nc = tc.nc
+
+    h_blocks = h2.flatten_outer_dims().rearrange("(n r s) d -> n r (s d)", r=P, s=SUB)
+    out_blocks = out.flatten_outer_dims().rearrange("(n r s) d -> n r (s d)", r=P, s=SUB)
+
+    with ExitStack() as whole:
+        keep = whole.enter_context(tc.tile_pool(name="keep", bufs=1))
+
+        ident = keep.tile([P, P], F32)
+        make_identity(nc, ident[:])
+        ones = keep.tile([P, P], F32)
+        nc.vector.memset(ones[:], 1.0)
+        eps_col = keep.tile([P, 1], F32)
+        nc.vector.memset(eps_col[:], EPS)
+        table_warm = keep.tile([P, 1], F32)
+        nc.scalar.activation(out=table_warm[:], in_=eps_col[:], func=ACT.Sqrt)
+
+        h_raw = keep.tile([P, N_BLOCKS, SUB * D], BF16)
+        h_grouped = keep.tile([P, N_BLOCKS, BLOCK, PACK], BF16, align_bytes=64)
+        t_cols = keep.tile([P, D_TILES, N_BLOCKS, BLOCK], F32)
+        w1_codes = keep.tile([P, F], U32, align_bytes=64)
+        w1_scales = keep.tile([P, F], U8, align_bytes=64)
+        w2_codes = keep.tile([P, F_PASSES, D], U32, align_bytes=64)
+        w2_scales = keep.tile([P, F_PASSES, D], U8, align_bytes=64)
+        b1_col = keep.tile([P, F_TILES], F32)
+        b2_col = keep.tile([P, D_TILES], F32)
+        sum_t = keep.tile([P, D_TILES * N_BLOCKS], F32)
+        sum_sq = keep.tile([P, D_TILES * N_BLOCKS], F32)
+
+        h_words = h_raw[:].bitcast(F32)
+        h_grouped_words = h_grouped[:].bitcast(F32)
+
+        with ExitStack() as layers:
+            wstage = layers.enter_context(tc.tile_pool(name="wstage", bufs=1))
+            work = layers.enter_context(tc.tile_pool(name="work", bufs=2))
+            psum_xt = layers.enter_context(tc.psum_pool(name="psum_xt", bufs=2))
+            psum_a = layers.enter_context(tc.psum_pool(name="psum_a", bufs=4))
+            psum_t = layers.enter_context(tc.psum_pool(name="psum_t", bufs=2))
+
+            w1_raw = wstage.tile([P, F_TILES, D], BF16)
+            nc.sync.dma_start(
+                out=w1_raw[:].rearrange("m (c e) d -> m c (e d)", e=2),
+                in_=w_ff1.rearrange("(c m e) d -> m c (e d)", m=P, e=2),
+            )
+            nc.sync.dma_start(out=h_raw[:, 0, :], in_=h_blocks[0])
+            nc.sync.dma_start(out=h_raw[:, 1, :], in_=h_blocks[1])
+            w2_raw = wstage.tile([P, D_TILES, F], BF16)
+            nc.sync.dma_start(
+                out=w2_raw[:].rearrange("m (u e) f -> m u (e f)", e=2),
+                in_=w_ff2.rearrange("(u m e) f -> m u (e f)", m=P, e=2),
+            )
+            for n in range(2, N_BLOCKS):
+                nc.sync.dma_start(out=h_raw[:, n, :], in_=h_blocks[n])
+
+            b1_bf = wstage.tile([P, F_TILES], BF16)
+            nc.scalar.dma_start(
+                out=b1_bf[:].rearrange("m (c e) -> m c e", e=2),
+                in_=b_ff1.rearrange("(c m e) -> m c e", m=P, e=2),
+            )
+            b2_bf = wstage.tile([P, D_TILES], BF16)
+            nc.scalar.dma_start(
+                out=b2_bf[:].rearrange("m (u e) -> m u e", e=2),
+                in_=b_ff2.rearrange("(u m e) -> m u e", m=P, e=2),
+            )
+            nc.vector.tensor_copy(out=b1_col[:], in_=b1_bf[:])
+            nc.vector.tensor_copy(out=b2_col[:], in_=b2_bf[:])
+
+            def copy_out(piece, dst, src):
+                if piece % 2 == 0:
+                    nc.scalar.copy(out=dst, in_=src)
+                else:
+                    nc.vector.tensor_copy(out=dst, in_=src)
+
+            w1_words = w1_raw[:].bitcast(F32)
+            w1_grouped = wstage.tile([P, F_TILES, P, PACK], BF16, align_bytes=64)
+            w1_grouped_words = w1_grouped[:].bitcast(F32)
+            for pair in range(F_TILES // 2):
+                bank = psum_xt.tile([P, 2, 2, P], F32, tag="xt")
+                for i in range(2):
+                    for u in range(2):
+                        nc.tensor.transpose(
+                            bank[:, i, u, :], w1_words[:, 2 * pair + i, u * P : (u + 1) * P], ident[:]
+                        )
+                copy_out(
+                    pair,
+                    w1_grouped_words[:, 2 * pair : 2 * pair + 2, :, :],
+                    bank[:].rearrange("p i u m -> p i m u"),
+                )
+            nc.vector.quantize_mx(
+                out=w1_codes[:].bitcast(FP8X4),
+                scales=w1_scales[:],
+                in_=w1_grouped[:].rearrange("p i m t -> p (i m t)"),
+            )
+
+            def pack_h(n):
+                for half in range(2):
+                    bank = psum_xt.tile([P, 2, 2, P], F32, tag="xt")
+                    for s in range(2):
+                        for u in range(2):
+                            first = (2 * (2 * half + s) + u) * P
+                            nc.tensor.transpose(
+                                bank[:, s, u, :], h_words[:, n, first : first + P], ident[:]
+                            )
+                    cols = slice(2 * half * P, 2 * (half + 1) * P)
+                    copy_out(
+                        half,
+                        h_grouped_words[:, n, cols, :].rearrange("p (s r) u -> p s r u", s=2),
+                        bank[:].rearrange("p s u r -> p s r u"),
+                    )
+                h_codes = work.tile([P, BLOCK], U32, align_bytes=64)
+                h_scales = work.tile([P, BLOCK], U8, align_bytes=64)
+                nc.vector.quantize_mx(
+                    out=h_codes[:].bitcast(FP8X4),
+                    scales=h_scales[:],
+                    in_=h_grouped[:, n, :, :].rearrange("p c t -> p (c t)"),
+                )
+                return h_codes, h_scales
+
+            def pack_w2():
+                w2_words = w2_raw[:].bitcast(F32)
+                w2_grouped = wstage.tile([P, F_PASSES, D_TILES, P, PACK], BF16, align_bytes=64)
+                w2_grouped_words = w2_grouped[:].bitcast(F32)
+                for j in range(D_TILES):
+                    bank = psum_xt.tile([P, 2 * F_PASSES, P], F32, tag="xt")
+                    for gu in range(2 * F_PASSES):
+                        nc.tensor.transpose(
+                            bank[:, gu, :], w2_words[:, j, gu * P : (gu + 1) * P], ident[:]
+                        )
+                    copy_out(
+                        j,
+                        w2_grouped_words[:, :, j, :, :],
+                        bank[:].rearrange("p (g u) m -> p g m u", u=2),
+                    )
+                nc.vector.quantize_mx(
+                    out=w2_codes[:].rearrange("p g c -> p (g c)").bitcast(FP8X4),
+                    scales=w2_scales[:].rearrange("p g c -> p (g c)"),
+                    in_=w2_grouped[:].rearrange("p g j m t -> p (g j m t)"),
+                )
+
+            def first_layer(h_codes, h_scales):
+                a_rows = work.tile([P, F_TILES, BLOCK], BF16)
+                for i in range(F_TILES):
+                    acc = psum_a.tile([P, BLOCK], F32, tag="acc_a")
+                    rows = slice(i * P, (i + 1) * P)
+                    nc.tensor.matmul_mx(
+                        out=acc[:],
+                        lhsT=w1_codes[:, rows].bitcast(FP8X4),
+                        lhsT_scale=w1_scales[:, rows],
+                        rhs=h_codes[:].bitcast(FP8X4),
+                        rhs_scale=h_scales[:],
+                        start=True,
+                        stop=True,
+                    )
+                    nc.scalar.activation(
+                        out=a_rows[:, i, :], in_=acc[:], func=ACT.Relu, bias=b1_col[:, i : i + 1]
+                    )
+                a_grouped = work.tile([P, F_PASSES, BLOCK, PACK], BF16, align_bytes=64)
+                for g in range(F_PASSES):
+                    nc.vector.tensor_copy(
+                        out=a_grouped[:, g, :, :].rearrange("p (c i) t -> p c t i", i=4),
+                        in_=a_rows[:, g * PACK : (g + 1) * PACK, :].rearrange(
+                            "p t (c i) -> p c t i", i=4
+                        ),
+                    )
+                a_codes = work.tile([P, F_PASSES, BLOCK], U32, align_bytes=64)
+                a_scales = work.tile([P, F_PASSES, BLOCK], U8, align_bytes=64)
+                for g in range(F_PASSES):
+                    nc.vector.quantize_mx(
+                        out=a_codes[:, g, :].bitcast(FP8X4),
+                        scales=a_scales[:, g, :],
+                        in_=a_grouped[:, g, :, :].rearrange("p c t -> p (c t)"),
+                    )
+                return a_codes, a_scales
+
+            def second_layer(n, a_codes, a_scales):
+                for j in range(D_TILES):
+                    acc = psum_t.tile([P, BLOCK], F32, tag="acc_t")
+                    rows = slice(j * P, (j + 1) * P)
+                    for g in range(F_PASSES):
+                        nc.tensor.matmul_mx(
+                            out=acc[:],
+                            lhsT=w2_codes[:, g, rows].bitcast(FP8X4),
+                            lhsT_scale=w2_scales[:, g, rows],
+                            rhs=a_codes[:, g, :].bitcast(FP8X4),
+                            rhs_scale=a_scales[:, g, :],
+                            start=(g == 0),
+                            stop=(g == F_PASSES - 1),
+                        )
+                    piece = n * D_TILES + j
+                    nc.vector.scalar_tensor_tensor(
+                        out=t_cols[:, j, n, :],
+                        in0=acc[:],
+                        scalar=b2_col[:, j : j + 1],
+                        in1=h_grouped[:, n, :, j],
+                        op0=ALU.add,
+                        op1=ALU.add,
+                        accum_out=sum_t[:, piece : piece + 1],
+                    )
+                    squares = work.tile([P, BLOCK], BF16)
+                    nc.scalar.activation(
+                        out=squares[:],
+                        in_=t_cols[:, j, n, :],
+                        func=ACT.Square,
+                        accum_out=sum_sq[:, piece : piece + 1],
+                    )
+
+            packed_h = {}
+            packed_a = {}
+            for step in range(N_BLOCKS + 2):
+                if step < N_BLOCKS:
+                    packed_h[step] = pack_h(step)
+                if step == 1:
+                    pack_w2()
+                if 1 <= step <= N_BLOCKS:
+                    packed_a[step - 1] = first_layer(*packed_h[step - 1])
+                if step >= 2:
+                    second_layer(step - 2, *packed_a[step - 2])
+
+        with ExitStack() as norm:
+            small = norm.enter_context(tc.tile_pool(name="small", bufs=1))
+            store = norm.enter_context(tc.tile_pool(name="store", bufs=3))
+            psum_tot = norm.enter_context(tc.psum_pool(name="psum_tot", bufs=1, reuse_waits="tile"))
+            psum_back = norm.enter_context(tc.psum_pool(name="psum_back", bufs=7, reuse_waits="tile"))
+
+            stat = small.tile([P, 2], F32)
+            nc.vector.tensor_reduce(out=stat[:, 0:1], in_=sum_t[:], axis=mybir.AxisListType.X, op=ALU.add)
+            nc.vector.tensor_reduce(out=stat[:, 1:2], in_=sum_sq[:], axis=mybir.AxisListType.X, op=ALU.add)
+            total = psum_tot.tile([P, 2], F32)
+            nc.tensor.matmul(out=total[:], lhsT=ones[:], rhs=stat[:], start=True, stop=True)
+            moments = small.tile([P, 2], F32)
+            nc.vector.tensor_scalar(
+                out=moments[:], in0=total[:], scalar1=1.0 / (TOKENS * D), scalar2=None, op0=ALU.mult
+            )
+            minus_var = small.tile([P, 1], F32)
+            nc.vector.scalar_tensor_tensor(
+                out=minus_var[:],
+                in0=moments[:, 0:1],
+                scalar=moments[:, 0:1],
+                in1=moments[:, 1:2],
+                op0=ALU.mult,
+                op1=ALU.subtract,
+            )
+            std = small.tile([P, 1], F32)
+            nc.scalar.activation(out=std[:], in_=minus_var[:], func=ACT.Sqrt, scale=-1.0, bias=eps_col[:])
+            rstd = small.tile([P, 1], F32)
+            nc.vector.reciprocal(out=rstd[:], in_=std[:])
+            shift = small.tile([P, 1], F32)
+            nc.vector.scalar_tensor_tensor(
+                out=shift[:], in0=moments[:, 0:1], scalar=-1.0, in1=rstd[:], op0=ALU.mult, op1=ALU.mult
+            )
+
+            for n in range(N_BLOCKS):
+                o_rows = store.tile([P, SUB, D], F32)
+                for s in range(SUB):
+                    bank = psum_back.tile([P, D_TILES, P], F32, tag="back")
+                    for j in range(D_TILES):
+                        nc.tensor.transpose(
+                            bank[:, j, :], t_cols[:, j, n, s * P : (s + 1) * P], ident[:]
+                        )
+                    src = bank[:].rearrange("r (u e) m -> r u m e", e=2)
+                    dst = o_rows[:, s, :].rearrange("r (u m e) -> r u m e", u=2, e=2)
+                    if s % 2 == 0:
+                        nc.scalar.activation(
+                            out=dst, in_=src, func=ACT.Identity, scale=rstd[:], bias=shift[:]
+                        )
+                    else:
+                        nc.vector.tensor_scalar(
+                            out=dst, in0=src, scalar1=rstd[:], scalar2=shift[:], op0=ALU.mult, op1=ALU.add
+                        )
+                nc.sync.dma_start(out=out_blocks[n], in_=o_rows[:].rearrange("r s d -> r (s d)"))

@@ -10,6 +10,7 @@ U8 = mybir.dt.uint8
 FP8X4 = mybir.dt.float8_e4m3fn_x4
 ACT = mybir.ActivationFunctionType
 ALU = mybir.AluOpType
+AXIS_X = mybir.AxisListType.X
 
 P = 128
 PACK = 4
@@ -18,10 +19,15 @@ F = 1024
 TOKENS = 2 * 2048
 BLOCK = 512
 SUB = BLOCK // P
+SLAB = 2 * P
 N_BLOCKS = TOKENS // BLOCK
+N_SLABS = TOKENS // SLAB
 F_TILES = F // P
 D_TILES = D // P
 F_PASSES = F // (P * PACK)
+ROUNDS = N_BLOCKS * F_PASSES
+PAIR = D_TILES // F_PASSES
+BACK_BANKS = 7
 EPS = 1e-5
 
 FLOPS = 2 * TOKENS * D * F * 2
@@ -34,6 +40,7 @@ def tile_decoderblock_pb_t_kernel(tc, h2, w_ff1, b_ff1, w_ff2, b_ff2, out):
     out_blocks = out.flatten_outer_dims().rearrange("(n r s) d -> n r (s d)", r=P, s=SUB)
 
     with ExitStack() as whole:
+        whole.enter_context(tc.manual_schedule())
         keep = whole.enter_context(tc.tile_pool(name="keep", bufs=1))
 
         ident = keep.tile([P, P], F32)
@@ -45,9 +52,11 @@ def tile_decoderblock_pb_t_kernel(tc, h2, w_ff1, b_ff1, w_ff2, b_ff2, out):
         table_warm = keep.tile([P, 1], F32)
         nc.scalar.activation(out=table_warm[:], in_=eps_col[:], func=ACT.Sqrt)
 
-        h_raw = keep.tile([P, N_BLOCKS, SUB * D], BF16)
-        h_grouped = keep.tile([P, N_BLOCKS, BLOCK, PACK], BF16, align_bytes=64)
-        t_cols = keep.tile([P, D_TILES, N_BLOCKS, BLOCK], F32)
+        h_raw = keep.tile([P, N_SLABS, 2 * D], BF16)
+        h_grouped = keep.tile([P, TOKENS, PACK], BF16, align_bytes=64)
+        h_codes = keep.tile([P, TOKENS], U32, align_bytes=64)
+        h_scales = keep.tile([P, TOKENS], U8, align_bytes=64)
+        t_cols = keep.tile([P, D_TILES, TOKENS], F32)
         w1_codes = keep.tile([P, F], U32, align_bytes=64)
         w1_scales = keep.tile([P, F], U8, align_bytes=64)
         w2_codes = keep.tile([P, F_PASSES, D], U32, align_bytes=64)
@@ -63,24 +72,31 @@ def tile_decoderblock_pb_t_kernel(tc, h2, w_ff1, b_ff1, w_ff2, b_ff2, out):
         with ExitStack() as layers:
             wstage = layers.enter_context(tc.tile_pool(name="wstage", bufs=1))
             work = layers.enter_context(tc.tile_pool(name="work", bufs=2))
+            coded = layers.enter_context(tc.tile_pool(name="coded", bufs=4))
             psum_xt = layers.enter_context(tc.psum_pool(name="psum_xt", bufs=2))
-            psum_a = layers.enter_context(tc.psum_pool(name="psum_a", bufs=4))
-            psum_t = layers.enter_context(tc.psum_pool(name="psum_t", bufs=2))
+            psum_a = layers.enter_context(tc.psum_pool(name="psum_a", bufs=PACK))
+            psum_t = layers.enter_context(tc.psum_pool(name="psum_t", bufs=PAIR))
 
             w1_raw = wstage.tile([P, F_TILES, D], BF16)
             nc.sync.dma_start(
                 out=w1_raw[:].rearrange("m (c e) d -> m c (e d)", e=2),
                 in_=w_ff1.rearrange("(c m e) d -> m c (e d)", m=P, e=2),
             )
-            nc.sync.dma_start(out=h_raw[:, 0, :], in_=h_blocks[0])
-            nc.sync.dma_start(out=h_raw[:, 1, :], in_=h_blocks[1])
+
+            def load_h(n):
+                nc.sync.dma_start(
+                    out=h_raw[:, 2 * n : 2 * n + 2, :].rearrange("r y w -> r (y w)"), in_=h_blocks[n]
+                )
+
+            load_h(0)
+            load_h(1)
             w2_raw = wstage.tile([P, D_TILES, F], BF16)
             nc.sync.dma_start(
                 out=w2_raw[:].rearrange("m (u e) f -> m u (e f)", e=2),
                 in_=w_ff2.rearrange("(u m e) f -> m u (e f)", m=P, e=2),
             )
             for n in range(2, N_BLOCKS):
-                nc.sync.dma_start(out=h_raw[:, n, :], in_=h_blocks[n])
+                load_h(n)
 
             b1_bf = wstage.tile([P, F_TILES], BF16)
             nc.scalar.dma_start(
@@ -105,7 +121,7 @@ def tile_decoderblock_pb_t_kernel(tc, h2, w_ff1, b_ff1, w_ff2, b_ff2, out):
             w1_grouped = wstage.tile([P, F_TILES, P, PACK], BF16, align_bytes=64)
             w1_grouped_words = w1_grouped[:].bitcast(F32)
             for pair in range(F_TILES // 2):
-                bank = psum_xt.tile([P, 2, 2, P], F32, tag="xt")
+                bank = psum_a.tile([P, 2, 2, P], F32, tag="acc_a")
                 for i in range(2):
                     for u in range(2):
                         nc.tensor.transpose(
@@ -119,39 +135,15 @@ def tile_decoderblock_pb_t_kernel(tc, h2, w_ff1, b_ff1, w_ff2, b_ff2, out):
             nc.vector.quantize_mx(
                 out=w1_codes[:].bitcast(FP8X4),
                 scales=w1_scales[:],
-                in_=w1_grouped[:].rearrange("p i m t -> p (i m t)"),
+                in_=w1_grouped[:].rearrange("p i m v -> p (i m v)"),
             )
-
-            def pack_h(n):
-                for half in range(2):
-                    bank = psum_xt.tile([P, 2, 2, P], F32, tag="xt")
-                    for s in range(2):
-                        for u in range(2):
-                            first = (2 * (2 * half + s) + u) * P
-                            nc.tensor.transpose(
-                                bank[:, s, u, :], h_words[:, n, first : first + P], ident[:]
-                            )
-                    cols = slice(2 * half * P, 2 * (half + 1) * P)
-                    copy_out(
-                        half,
-                        h_grouped_words[:, n, cols, :].rearrange("p (s r) u -> p s r u", s=2),
-                        bank[:].rearrange("p s u r -> p s r u"),
-                    )
-                h_codes = work.tile([P, BLOCK], U32, align_bytes=64)
-                h_scales = work.tile([P, BLOCK], U8, align_bytes=64)
-                nc.vector.quantize_mx(
-                    out=h_codes[:].bitcast(FP8X4),
-                    scales=h_scales[:],
-                    in_=h_grouped[:, n, :, :].rearrange("p c t -> p (c t)"),
-                )
-                return h_codes, h_scales
 
             def pack_w2():
                 w2_words = w2_raw[:].bitcast(F32)
                 w2_grouped = wstage.tile([P, F_PASSES, D_TILES, P, PACK], BF16, align_bytes=64)
                 w2_grouped_words = w2_grouped[:].bitcast(F32)
                 for j in range(D_TILES):
-                    bank = psum_xt.tile([P, 2 * F_PASSES, P], F32, tag="xt")
+                    bank = psum_t.tile([P, 2 * F_PASSES, P], F32, tag="acc_t")
                     for gu in range(2 * F_PASSES):
                         nc.tensor.transpose(
                             bank[:, gu, :], w2_words[:, j, gu * P : (gu + 1) * P], ident[:]
@@ -164,97 +156,168 @@ def tile_decoderblock_pb_t_kernel(tc, h2, w_ff1, b_ff1, w_ff2, b_ff2, out):
                 nc.vector.quantize_mx(
                     out=w2_codes[:].rearrange("p g c -> p (g c)").bitcast(FP8X4),
                     scales=w2_scales[:].rearrange("p g c -> p (g c)"),
-                    in_=w2_grouped[:].rearrange("p g j m t -> p (g j m t)"),
+                    in_=w2_grouped[:].rearrange("p g j m v -> p (g j m v)"),
                 )
 
-            def first_layer(h_codes, h_scales):
-                a_rows = work.tile([P, F_TILES, BLOCK], BF16)
-                for i in range(F_TILES):
-                    acc = psum_a.tile([P, BLOCK], F32, tag="acc_a")
-                    rows = slice(i * P, (i + 1) * P)
-                    nc.tensor.matmul_mx(
-                        out=acc[:],
-                        lhsT=w1_codes[:, rows].bitcast(FP8X4),
-                        lhsT_scale=w1_scales[:, rows],
-                        rhs=h_codes[:].bitcast(FP8X4),
-                        rhs_scale=h_scales[:],
-                        start=True,
-                        stop=True,
-                    )
-                    nc.scalar.activation(
-                        out=a_rows[:, i, :], in_=acc[:], func=ACT.Relu, bias=b1_col[:, i : i + 1]
-                    )
-                a_grouped = work.tile([P, F_PASSES, BLOCK, PACK], BF16, align_bytes=64)
-                for g in range(F_PASSES):
-                    nc.vector.tensor_copy(
-                        out=a_grouped[:, g, :, :].rearrange("p (c i) t -> p c t i", i=4),
-                        in_=a_rows[:, g * PACK : (g + 1) * PACK, :].rearrange(
-                            "p t (c i) -> p c t i", i=4
-                        ),
-                    )
-                a_codes = work.tile([P, F_PASSES, BLOCK], U32, align_bytes=64)
-                a_scales = work.tile([P, F_PASSES, BLOCK], U8, align_bytes=64)
-                for g in range(F_PASSES):
-                    nc.vector.quantize_mx(
-                        out=a_codes[:, g, :].bitcast(FP8X4),
-                        scales=a_scales[:, g, :],
-                        in_=a_grouped[:, g, :, :].rearrange("p c t -> p (c t)"),
-                    )
-                return a_codes, a_scales
+            xt_banks = {}
+            a_banks = {}
+            a_rows = {}
+            a_grouped = {}
+            a_codes = {}
+            a_scales = {}
+            t_banks = {}
 
-            def second_layer(n, a_codes, a_scales):
-                for j in range(D_TILES):
-                    acc = psum_t.tile([P, BLOCK], F32, tag="acc_t")
+            def transpose_h(y):
+                xt_banks[y] = psum_xt.tile([P, 4, P], F32, tag="xt", name="xt_bank")
+                for su in range(4):
+                    nc.tensor.transpose(
+                        xt_banks[y][:, su, :], h_words[:, y, su * P : (su + 1) * P], ident[:]
+                    )
+
+            def group_h(y):
+                cols = slice(y * SLAB, (y + 1) * SLAB)
+                copy_out(
+                    y,
+                    h_grouped_words[:, cols, :].rearrange("p (s r) u -> p s r u", s=2),
+                    xt_banks[y][:].rearrange("p (s u) r -> p s r u", u=2),
+                )
+
+            def quantise_h(y):
+                cols = slice(y * SLAB, (y + 1) * SLAB)
+                nc.vector.quantize_mx(
+                    out=h_codes[:, cols].bitcast(FP8X4),
+                    scales=h_scales[:, cols],
+                    in_=h_grouped[:, cols, :].rearrange("p c v -> p (c v)"),
+                )
+
+            def first_product(x, v):
+                n, g = divmod(x, F_PASSES)
+                rows = slice((g * PACK + v) * P, (g * PACK + v + 1) * P)
+                cols = slice(n * BLOCK, (n + 1) * BLOCK)
+                a_banks[x, v] = psum_a.tile([P, BLOCK], F32, tag="acc_a", name="a_bank")
+                nc.tensor.matmul_mx(
+                    out=a_banks[x, v][:],
+                    lhsT=w1_codes[:, rows].bitcast(FP8X4),
+                    lhsT_scale=w1_scales[:, rows],
+                    rhs=h_codes[:, cols].bitcast(FP8X4),
+                    rhs_scale=h_scales[:, cols],
+                    start=True,
+                    stop=True,
+                )
+
+            def relu_out(x, v):
+                if v == 0:
+                    a_rows[x] = work.tile([P, PACK, BLOCK], BF16, name="a_rows")
+                i = (x % F_PASSES) * PACK + v
+                nc.scalar.activation(
+                    out=a_rows[x][:, v, :], in_=a_banks[x, v][:], func=ACT.Relu, bias=b1_col[:, i : i + 1]
+                )
+
+            def group_a(x):
+                a_grouped[x] = work.tile([P, BLOCK, PACK], BF16, align_bytes=64, name="a_grouped")
+                nc.vector.tensor_copy(
+                    out=a_grouped[x][:].rearrange("p (c i) v -> p c v i", i=4),
+                    in_=a_rows[x][:].rearrange("p v (c i) -> p c v i", i=4),
+                )
+
+            def quantise_a(x):
+                a_codes[x] = coded.tile([P, BLOCK], U32, align_bytes=64, name="a_codes")
+                a_scales[x] = coded.tile([P, BLOCK], U8, align_bytes=64, name="a_scales")
+                nc.vector.quantize_mx(
+                    out=a_codes[x][:].bitcast(FP8X4),
+                    scales=a_scales[x][:],
+                    in_=a_grouped[x][:].rearrange("p c v -> p (c v)"),
+                )
+
+            def second_product(x):
+                n, pair = divmod(x, F_PASSES)
+                for j in range(pair * PAIR, (pair + 1) * PAIR):
                     rows = slice(j * P, (j + 1) * P)
+                    t_banks[n, j] = psum_t.tile([P, BLOCK], F32, tag="acc_t", name="t_bank")
                     for g in range(F_PASSES):
                         nc.tensor.matmul_mx(
-                            out=acc[:],
+                            out=t_banks[n, j][:],
                             lhsT=w2_codes[:, g, rows].bitcast(FP8X4),
                             lhsT_scale=w2_scales[:, g, rows],
-                            rhs=a_codes[:, g, :].bitcast(FP8X4),
-                            rhs_scale=a_scales[:, g, :],
+                            rhs=a_codes[n * F_PASSES + g][:].bitcast(FP8X4),
+                            rhs_scale=a_scales[n * F_PASSES + g][:],
                             start=(g == 0),
                             stop=(g == F_PASSES - 1),
                         )
-                    piece = n * D_TILES + j
+
+            def add_residual(x):
+                n, pair = divmod(x, F_PASSES)
+                cols = slice(n * BLOCK, (n + 1) * BLOCK)
+                for j in range(pair * PAIR, (pair + 1) * PAIR):
                     nc.vector.scalar_tensor_tensor(
-                        out=t_cols[:, j, n, :],
-                        in0=acc[:],
+                        out=t_cols[:, j, cols],
+                        in0=t_banks[n, j][:],
                         scalar=b2_col[:, j : j + 1],
-                        in1=h_grouped[:, n, :, j],
+                        in1=h_grouped[:, cols, j],
                         op0=ALU.add,
                         op1=ALU.add,
-                        accum_out=sum_t[:, piece : piece + 1],
+                        accum_out=sum_t[:, n * D_TILES + j : n * D_TILES + j + 1],
                     )
+
+            def square(x):
+                n, pair = divmod(x, F_PASSES)
+                cols = slice(n * BLOCK, (n + 1) * BLOCK)
+                for j in range(pair * PAIR, (pair + 1) * PAIR):
                     squares = work.tile([P, BLOCK], BF16)
                     nc.scalar.activation(
                         out=squares[:],
-                        in_=t_cols[:, j, n, :],
+                        in_=t_cols[:, j, cols],
                         func=ACT.Square,
-                        accum_out=sum_sq[:, piece : piece + 1],
+                        accum_out=sum_sq[:, n * D_TILES + j : n * D_TILES + j + 1],
                     )
 
-            packed_h = {}
-            packed_a = {}
-            for step in range(N_BLOCKS + 2):
-                if step < N_BLOCKS:
-                    packed_h[step] = pack_h(step)
-                if step == 1:
+            for x in range(-5, ROUNDS + 3):
+                if 0 <= x - 3 < ROUNDS:
+                    add_residual(x - 3)
+                if 0 <= x - 1 < ROUNDS:
+                    quantise_a(x - 1)
+                if x == 1:
                     pack_w2()
-                if 1 <= step <= N_BLOCKS:
-                    packed_a[step - 1] = first_layer(*packed_h[step - 1])
-                if step >= 2:
-                    second_layer(step - 2, *packed_a[step - 2])
+                for v in range(PACK):
+                    if 0 <= x < ROUNDS:
+                        relu_out(x, v)
+                    if 0 <= x + 1 < ROUNDS:
+                        first_product(x + 1, v)
+                if 0 <= x - 2 < ROUNDS:
+                    second_product(x - 2)
+                if 0 <= x + 5 < N_SLABS:
+                    transpose_h(x + 5)
+                if 0 <= x + 4 < N_SLABS:
+                    group_h(x + 4)
+                if 0 <= x + 3 < N_SLABS:
+                    quantise_h(x + 3)
+                if 0 <= x < ROUNDS:
+                    group_a(x)
+                if 0 <= x - 3 < ROUNDS:
+                    square(x - 3)
 
         with ExitStack() as norm:
             small = norm.enter_context(tc.tile_pool(name="small", bufs=1))
-            store = norm.enter_context(tc.tile_pool(name="store", bufs=3))
+            store = norm.enter_context(tc.tile_pool(name="store", bufs=6))
             psum_tot = norm.enter_context(tc.psum_pool(name="psum_tot", bufs=1, reuse_waits="tile"))
-            psum_back = norm.enter_context(tc.psum_pool(name="psum_back", bufs=7, reuse_waits="tile"))
+            psum_back = norm.enter_context(
+                tc.psum_pool(name="psum_back", bufs=BACK_BANKS, reuse_waits="tile")
+            )
+            back_banks = {}
+
+            def transpose_back(q):
+                back_banks[q] = psum_back.tile([P, D_TILES, P], F32, tag="back", name="back_bank")
+                for j in range(D_TILES):
+                    nc.tensor.transpose(
+                        back_banks[q][:, j, :], t_cols[:, j, q * P : (q + 1) * P], ident[:]
+                    )
+
+            for q in range(BACK_BANKS):
+                transpose_back(q)
 
             stat = small.tile([P, 2], F32)
-            nc.vector.tensor_reduce(out=stat[:, 0:1], in_=sum_t[:], axis=mybir.AxisListType.X, op=ALU.add)
-            nc.vector.tensor_reduce(out=stat[:, 1:2], in_=sum_sq[:], axis=mybir.AxisListType.X, op=ALU.add)
+            nc.vector.tensor_reduce(out=stat[:, 0:1], in_=sum_t[:], axis=AXIS_X, op=ALU.add)
+            nc.vector.tensor_reduce(out=stat[:, 1:2], in_=sum_sq[:], axis=AXIS_X, op=ALU.add)
             total = psum_tot.tile([P, 2], F32)
             nc.tensor.matmul(out=total[:], lhsT=ones[:], rhs=stat[:], start=True, stop=True)
             moments = small.tile([P, 2], F32)
@@ -279,22 +342,21 @@ def tile_decoderblock_pb_t_kernel(tc, h2, w_ff1, b_ff1, w_ff2, b_ff2, out):
                 out=shift[:], in0=moments[:, 0:1], scalar=-1.0, in1=rstd[:], op0=ALU.mult, op1=ALU.mult
             )
 
-            for n in range(N_BLOCKS):
-                o_rows = store.tile([P, SUB, D], F32)
-                for s in range(SUB):
-                    bank = psum_back.tile([P, D_TILES, P], F32, tag="back")
-                    for j in range(D_TILES):
-                        nc.tensor.transpose(
-                            bank[:, j, :], t_cols[:, j, n, s * P : (s + 1) * P], ident[:]
-                        )
-                    src = bank[:].rearrange("r (u e) m -> r u m e", e=2)
-                    dst = o_rows[:, s, :].rearrange("r (u m e) -> r u m e", u=2, e=2)
-                    if s % 2 == 0:
-                        nc.scalar.activation(
-                            out=dst, in_=src, func=ACT.Identity, scale=rstd[:], bias=shift[:]
-                        )
-                    else:
-                        nc.vector.tensor_scalar(
-                            out=dst, in0=src, scalar1=rstd[:], scalar2=shift[:], op0=ALU.mult, op1=ALU.add
-                        )
-                nc.sync.dma_start(out=out_blocks[n], in_=o_rows[:].rearrange("r s d -> r (s d)"))
+            for q in range(TOKENS // P):
+                n, s = divmod(q, SUB)
+                if s % 2 == 0:
+                    o_rows = store.tile([P, 2, D], F32)
+                src = back_banks[q][:].rearrange("r (u e) m -> r u m e", e=2)
+                dst = o_rows[:, s % 2, :].rearrange("r (u m e) -> r u m e", u=2, e=2)
+                if s % 2 == 0:
+                    nc.scalar.activation(out=dst, in_=src, func=ACT.Identity, scale=rstd[:], bias=shift[:])
+                else:
+                    nc.vector.tensor_scalar(
+                        out=dst, in0=src, scalar1=rstd[:], scalar2=shift[:], op0=ALU.mult, op1=ALU.add
+                    )
+                    nc.sync.dma_start(
+                        out=out_blocks[n][:, (s - 1) * D : (s + 1) * D],
+                        in_=o_rows[:].rearrange("r s d -> r (s d)"),
+                    )
+                if q + BACK_BANKS < TOKENS // P:
+                    transpose_back(q + BACK_BANKS)

@@ -22,12 +22,14 @@ SUB = BLOCK // P
 SLAB = 2 * P
 N_BLOCKS = TOKENS // BLOCK
 N_SLABS = TOKENS // SLAB
+N_PIECES = TOKENS // P
 F_TILES = F // P
 D_TILES = D // P
 F_PASSES = F // (P * PACK)
 ROUNDS = N_BLOCKS * F_PASSES
-PAIR = D_TILES // F_PASSES
-BACK_BANKS = 7
+T_TILES = N_BLOCKS * D_TILES
+RING = 7
+AHEAD = 4
 EPS = 1e-5
 
 FLOPS = 2 * TOKENS * D * F * 2
@@ -52,36 +54,31 @@ def tile_decoderblock_pb_t_kernel(tc, h2, w_ff1, b_ff1, w_ff2, b_ff2, out):
         table_warm = keep.tile([P, 1], F32)
         nc.scalar.activation(out=table_warm[:], in_=eps_col[:], func=ACT.Sqrt)
 
-        h_raw = keep.tile([P, N_SLABS, 2 * D], BF16)
         h_grouped = keep.tile([P, TOKENS, PACK], BF16, align_bytes=64)
         h_codes = keep.tile([P, TOKENS], U32, align_bytes=64)
         h_scales = keep.tile([P, TOKENS], U8, align_bytes=64)
-        t_cols = keep.tile([P, D_TILES, TOKENS], F32)
-        w1_codes = keep.tile([P, F], U32, align_bytes=64)
-        w1_scales = keep.tile([P, F], U8, align_bytes=64)
-        w2_codes = keep.tile([P, F_PASSES, D], U32, align_bytes=64)
-        w2_scales = keep.tile([P, F_PASSES, D], U8, align_bytes=64)
+        a_codes = keep.tile([P, ROUNDS, BLOCK], U32, align_bytes=64)
+        a_scales = keep.tile([P, ROUNDS, BLOCK], U8, align_bytes=64)
+        w1_codes = keep.tile([P, F_TILES, P], U32, align_bytes=64)
+        w1_scales = keep.tile([P, F_TILES, P], U8, align_bytes=64)
+        w2_codes = keep.tile([P, D_TILES, F_PASSES, P], U32, align_bytes=64)
+        w2_scales = keep.tile([P, D_TILES, F_PASSES, P], U8, align_bytes=64)
         b1_col = keep.tile([P, F_TILES], F32)
         b2_col = keep.tile([P, D_TILES], F32)
-        sum_t = keep.tile([P, D_TILES * N_BLOCKS], F32)
-        sum_sq = keep.tile([P, D_TILES * N_BLOCKS], F32)
+        sum_t = keep.tile([P, T_TILES], F32)
+        sum_sq = keep.tile([P, T_TILES], F32)
 
-        h_words = h_raw[:].bitcast(F32)
         h_grouped_words = h_grouped[:].bitcast(F32)
 
-        with ExitStack() as layers:
-            wstage = layers.enter_context(tc.tile_pool(name="wstage", bufs=1))
-            work = layers.enter_context(tc.tile_pool(name="work", bufs=2))
-            coded = layers.enter_context(tc.tile_pool(name="coded", bufs=4))
-            psum_xt = layers.enter_context(tc.psum_pool(name="psum_xt", bufs=2))
-            psum_a = layers.enter_context(tc.psum_pool(name="psum_a", bufs=PACK))
-            psum_t = layers.enter_context(tc.psum_pool(name="psum_t", bufs=PAIR))
+        with ExitStack() as first:
+            stage = first.enter_context(tc.tile_pool(name="stage", bufs=1))
+            work = first.enter_context(tc.tile_pool(name="work", bufs=2))
+            psum_x = first.enter_context(tc.psum_pool(name="psum_x", bufs=4))
+            psum_a = first.enter_context(tc.psum_pool(name="psum_a", bufs=PACK))
 
-            w1_raw = wstage.tile([P, F_TILES, D], BF16)
-            nc.sync.dma_start(
-                out=w1_raw[:].rearrange("m (c e) d -> m c (e d)", e=2),
-                in_=w_ff1.rearrange("(c m e) d -> m c (e d)", m=P, e=2),
-            )
+            h_raw = stage.tile([P, N_SLABS, 2 * D], BF16)
+            w1_raw = stage.tile([P, F_TILES, D], BF16)
+            w2_raw = stage.tile([P, D_TILES, F], BF16)
 
             def load_h(n):
                 nc.sync.dma_start(
@@ -89,97 +86,56 @@ def tile_decoderblock_pb_t_kernel(tc, h2, w_ff1, b_ff1, w_ff2, b_ff2, out):
                 )
 
             load_h(0)
-            load_h(1)
-            w2_raw = wstage.tile([P, D_TILES, F], BF16)
+            for g in range(F_PASSES):
+                nc.sync.dma_start(
+                    out=w1_raw[:, g * PACK : (g + 1) * PACK, :].rearrange("m (u e) d -> m u (e d)", e=2),
+                    in_=w_ff1[g * P * PACK : (g + 1) * P * PACK, :].rearrange(
+                        "(u m e) d -> m u (e d)", m=P, e=2
+                    ),
+                )
+            for n in range(1, N_BLOCKS):
+                load_h(n)
             nc.sync.dma_start(
                 out=w2_raw[:].rearrange("m (u e) f -> m u (e f)", e=2),
                 in_=w_ff2.rearrange("(u m e) f -> m u (e f)", m=P, e=2),
             )
-            for n in range(2, N_BLOCKS):
-                load_h(n)
-
-            b1_bf = wstage.tile([P, F_TILES], BF16)
+            b1_bf = stage.tile([P, F_TILES], BF16)
             nc.scalar.dma_start(
                 out=b1_bf[:].rearrange("m (c e) -> m c e", e=2),
                 in_=b_ff1.rearrange("(c m e) -> m c e", m=P, e=2),
             )
-            b2_bf = wstage.tile([P, D_TILES], BF16)
+            b2_bf = stage.tile([P, D_TILES], BF16)
             nc.scalar.dma_start(
                 out=b2_bf[:].rearrange("m (u e) -> m u e", e=2),
                 in_=b_ff2.rearrange("(u m e) -> m u e", m=P, e=2),
             )
-            nc.vector.tensor_copy(out=b1_col[:], in_=b1_bf[:])
-            nc.vector.tensor_copy(out=b2_col[:], in_=b2_bf[:])
 
-            def copy_out(piece, dst, src):
-                if piece % 2 == 0:
-                    nc.scalar.copy(out=dst, in_=src)
-                else:
-                    nc.vector.tensor_copy(out=dst, in_=src)
-
+            h_words = h_raw[:].bitcast(F32)
             w1_words = w1_raw[:].bitcast(F32)
-            w1_grouped = wstage.tile([P, F_TILES, P, PACK], BF16, align_bytes=64)
+            w2_words = w2_raw[:].bitcast(F32)
+            w1_grouped = stage.tile([P, F_TILES, P, PACK], BF16, align_bytes=64)
             w1_grouped_words = w1_grouped[:].bitcast(F32)
-            for pair in range(F_TILES // 2):
-                bank = psum_a.tile([P, 2, 2, P], F32, tag="acc_a")
-                for i in range(2):
-                    for u in range(2):
-                        nc.tensor.transpose(
-                            bank[:, i, u, :], w1_words[:, 2 * pair + i, u * P : (u + 1) * P], ident[:]
-                        )
-                copy_out(
-                    pair,
-                    w1_grouped_words[:, 2 * pair : 2 * pair + 2, :, :],
-                    bank[:].rearrange("p i u m -> p i m u"),
-                )
-            nc.vector.quantize_mx(
-                out=w1_codes[:].bitcast(FP8X4),
-                scales=w1_scales[:],
-                in_=w1_grouped[:].rearrange("p i m v -> p (i m v)"),
-            )
+            w2_grouped = stage.tile([P, D_TILES, F_PASSES, P, PACK], BF16, align_bytes=64)
+            w2_grouped_words = w2_grouped[:].bitcast(F32)
 
-            def pack_w2():
-                w2_words = w2_raw[:].bitcast(F32)
-                w2_grouped = wstage.tile([P, F_PASSES, D_TILES, P, PACK], BF16, align_bytes=64)
-                w2_grouped_words = w2_grouped[:].bitcast(F32)
-                for j in range(D_TILES):
-                    bank = psum_t.tile([P, 2 * F_PASSES, P], F32, tag="acc_t")
-                    for gu in range(2 * F_PASSES):
-                        nc.tensor.transpose(
-                            bank[:, gu, :], w2_words[:, j, gu * P : (gu + 1) * P], ident[:]
-                        )
-                    copy_out(
-                        j,
-                        w2_grouped_words[:, :, j, :, :],
-                        bank[:].rearrange("p (g u) m -> p g m u", u=2),
-                    )
-                nc.vector.quantize_mx(
-                    out=w2_codes[:].rearrange("p g c -> p (g c)").bitcast(FP8X4),
-                    scales=w2_scales[:].rearrange("p g c -> p (g c)"),
-                    in_=w2_grouped[:].rearrange("p g j m v -> p (g j m v)"),
-                )
-
-            xt_banks = {}
+            x_banks = {}
             a_banks = {}
             a_rows = {}
             a_grouped = {}
-            a_codes = {}
-            a_scales = {}
-            t_banks = {}
+
+            def transpose_words(key, words):
+                x_banks[key] = psum_x.tile([P, 4, P], F32, tag="x", name="x_bank")
+                for k in range(4):
+                    nc.tensor.transpose(x_banks[key][:, k, :], words[:, k * P : (k + 1) * P], ident[:])
 
             def transpose_h(y):
-                xt_banks[y] = psum_xt.tile([P, 4, P], F32, tag="xt", name="xt_bank")
-                for su in range(4):
-                    nc.tensor.transpose(
-                        xt_banks[y][:, su, :], h_words[:, y, su * P : (su + 1) * P], ident[:]
-                    )
+                transpose_words(("h", y), h_words[:, y, :])
 
             def group_h(y):
                 cols = slice(y * SLAB, (y + 1) * SLAB)
-                copy_out(
-                    y,
-                    h_grouped_words[:, cols, :].rearrange("p (s r) u -> p s r u", s=2),
-                    xt_banks[y][:].rearrange("p (s u) r -> p s r u", u=2),
+                nc.vector.tensor_copy(
+                    out=h_grouped_words[:, cols, :].rearrange("p (s r) u -> p s r u", s=2),
+                    in_=x_banks["h", y][:].rearrange("p (s u) r -> p s r u", u=2),
                 )
 
             def quantise_h(y):
@@ -190,15 +146,43 @@ def tile_decoderblock_pb_t_kernel(tc, h2, w_ff1, b_ff1, w_ff2, b_ff2, out):
                     in_=h_grouped[:, cols, :].rearrange("p c v -> p (c v)"),
                 )
 
+            def pack_w1(g):
+                tiles = slice(g * PACK, (g + 1) * PACK)
+                for i in range(g * PACK, (g + 1) * PACK, 2):
+                    transpose_words(("w1", i), w1_words[:, i : i + 2, :].rearrange("m i w -> m (i w)"))
+                for i in range(g * PACK, (g + 1) * PACK, 2):
+                    nc.scalar.copy(
+                        out=w1_grouped_words[:, i : i + 2, :, :],
+                        in_=x_banks["w1", i][:].rearrange("p (i u) m -> p i m u", u=2),
+                    )
+                nc.vector.quantize_mx(
+                    out=w1_codes[:, tiles, :].rearrange("p i m -> p (i m)").bitcast(FP8X4),
+                    scales=w1_scales[:, tiles, :].rearrange("p i m -> p (i m)"),
+                    in_=w1_grouped[:, tiles, :, :].rearrange("p i m v -> p (i m v)"),
+                )
+
+            def pack_w2():
+                for j in range(D_TILES):
+                    transpose_words(("w2", j), w2_words[:, j, :])
+                for j in range(D_TILES):
+                    nc.scalar.copy(
+                        out=w2_grouped_words[:, j, :, :, :],
+                        in_=x_banks["w2", j][:].rearrange("p (g u) m -> p g m u", u=2),
+                    )
+                    nc.vector.quantize_mx(
+                        out=w2_codes[:, j, :, :].rearrange("p g m -> p (g m)").bitcast(FP8X4),
+                        scales=w2_scales[:, j, :, :].rearrange("p g m -> p (g m)"),
+                        in_=w2_grouped[:, j, :, :, :].rearrange("p g m v -> p (g m v)"),
+                    )
+
             def first_product(x, v):
                 n, g = divmod(x, F_PASSES)
-                rows = slice((g * PACK + v) * P, (g * PACK + v + 1) * P)
                 cols = slice(n * BLOCK, (n + 1) * BLOCK)
-                a_banks[x, v] = psum_a.tile([P, BLOCK], F32, tag="acc_a", name="a_bank")
+                a_banks[x, v] = psum_a.tile([P, BLOCK], F32, tag="a", name="a_bank")
                 nc.tensor.matmul_mx(
                     out=a_banks[x, v][:],
-                    lhsT=w1_codes[:, rows].bitcast(FP8X4),
-                    lhsT_scale=w1_scales[:, rows],
+                    lhsT=w1_codes[:, g * PACK + v, :].bitcast(FP8X4),
+                    lhsT_scale=w1_scales[:, g * PACK + v, :],
                     rhs=h_codes[:, cols].bitcast(FP8X4),
                     rhs_scale=h_scales[:, cols],
                     start=True,
@@ -221,110 +205,120 @@ def tile_decoderblock_pb_t_kernel(tc, h2, w_ff1, b_ff1, w_ff2, b_ff2, out):
                 )
 
             def quantise_a(x):
-                a_codes[x] = coded.tile([P, BLOCK], U32, align_bytes=64, name="a_codes")
-                a_scales[x] = coded.tile([P, BLOCK], U8, align_bytes=64, name="a_scales")
                 nc.vector.quantize_mx(
-                    out=a_codes[x][:].bitcast(FP8X4),
-                    scales=a_scales[x][:],
+                    out=a_codes[:, x, :].bitcast(FP8X4),
+                    scales=a_scales[:, x, :],
                     in_=a_grouped[x][:].rearrange("p c v -> p (c v)"),
                 )
 
-            def second_product(x):
-                n, pair = divmod(x, F_PASSES)
-                for j in range(pair * PAIR, (pair + 1) * PAIR):
-                    rows = slice(j * P, (j + 1) * P)
-                    t_banks[n, j] = psum_t.tile([P, BLOCK], F32, tag="acc_t", name="t_bank")
-                    for g in range(F_PASSES):
-                        nc.tensor.matmul_mx(
-                            out=t_banks[n, j][:],
-                            lhsT=w2_codes[:, g, rows].bitcast(FP8X4),
-                            lhsT_scale=w2_scales[:, g, rows],
-                            rhs=a_codes[n * F_PASSES + g][:].bitcast(FP8X4),
-                            rhs_scale=a_scales[n * F_PASSES + g][:],
-                            start=(g == 0),
-                            stop=(g == F_PASSES - 1),
-                        )
+            transpose_h(0)
+            transpose_h(1)
+            group_h(0)
+            group_h(1)
+            quantise_h(0)
+            quantise_h(1)
+            nc.vector.tensor_copy(out=b1_col[:], in_=b1_bf[:])
+            nc.vector.tensor_copy(out=b2_col[:], in_=b2_bf[:])
+            for g in range(F_PASSES):
+                pack_w1(g)
+            for v in range(PACK):
+                first_product(0, v)
 
-            def add_residual(x):
-                n, pair = divmod(x, F_PASSES)
-                cols = slice(n * BLOCK, (n + 1) * BLOCK)
-                for j in range(pair * PAIR, (pair + 1) * PAIR):
-                    nc.vector.scalar_tensor_tensor(
-                        out=t_cols[:, j, cols],
-                        in0=t_banks[n, j][:],
-                        scalar=b2_col[:, j : j + 1],
-                        in1=h_grouped[:, cols, j],
-                        op0=ALU.add,
-                        op1=ALU.add,
-                        accum_out=sum_t[:, n * D_TILES + j : n * D_TILES + j + 1],
-                    )
-
-            def square(x):
-                n, pair = divmod(x, F_PASSES)
-                cols = slice(n * BLOCK, (n + 1) * BLOCK)
-                for j in range(pair * PAIR, (pair + 1) * PAIR):
-                    squares = work.tile([P, BLOCK], BF16)
-                    nc.scalar.activation(
-                        out=squares[:],
-                        in_=t_cols[:, j, cols],
-                        func=ACT.Square,
-                        accum_out=sum_sq[:, n * D_TILES + j : n * D_TILES + j + 1],
-                    )
-
-            for x in range(-5, ROUNDS + 3):
-                if 0 <= x - 3 < ROUNDS:
-                    add_residual(x - 3)
-                if 0 <= x - 1 < ROUNDS:
+            for x in range(-3, ROUNDS):
+                if 0 <= x - 1:
                     quantise_a(x - 1)
-                if x == 1:
-                    pack_w2()
-                for v in range(PACK):
-                    if 0 <= x < ROUNDS:
-                        relu_out(x, v)
-                    if 0 <= x + 1 < ROUNDS:
-                        first_product(x + 1, v)
-                if 0 <= x - 2 < ROUNDS:
-                    second_product(x - 2)
-                if 0 <= x + 5 < N_SLABS:
-                    transpose_h(x + 5)
-                if 0 <= x + 4 < N_SLABS:
-                    group_h(x + 4)
-                if 0 <= x + 3 < N_SLABS:
+                if 2 <= x + 3 < N_SLABS:
                     quantise_h(x + 3)
-                if 0 <= x < ROUNDS:
+                for v in range(PACK):
+                    if 0 <= x:
+                        relu_out(x, v)
+                    if 1 <= x + 1 < ROUNDS:
+                        first_product(x + 1, v)
+                if 2 <= x + 5 < N_SLABS:
+                    transpose_h(x + 5)
+                if 0 <= x:
                     group_a(x)
-                if 0 <= x - 3 < ROUNDS:
-                    square(x - 3)
+                if 2 <= x + 4 < N_SLABS:
+                    group_h(x + 4)
 
-        with ExitStack() as norm:
-            small = norm.enter_context(tc.tile_pool(name="small", bufs=1))
-            store = norm.enter_context(tc.tile_pool(name="store", bufs=6))
-            psum_tot = norm.enter_context(tc.psum_pool(name="psum_tot", bufs=1, reuse_waits="tile"))
-            psum_back = norm.enter_context(
-                tc.psum_pool(name="psum_back", bufs=BACK_BANKS, reuse_waits="tile")
-            )
+            pack_w2()
+            quantise_a(ROUNDS - 1)
+
+        with ExitStack() as rest:
+            late = rest.enter_context(tc.tile_pool(name="late", bufs=1))
+            scratch = rest.enter_context(tc.tile_pool(name="scratch", bufs=2))
+            store = rest.enter_context(tc.tile_pool(name="store", bufs=6))
+            psum_tot = rest.enter_context(tc.psum_pool(name="psum_tot", bufs=1, reuse_waits="tile"))
+            psum_ring = rest.enter_context(tc.psum_pool(name="psum_ring", bufs=RING, reuse_waits="tile"))
+
+            t_cols = late.tile([P, D_TILES, TOKENS], F32)
+            t_banks = {}
             back_banks = {}
 
+            def second_product(z):
+                n, j = divmod(z, D_TILES)
+                t_banks[z] = psum_ring.tile([P, BLOCK], F32, tag="ring", name="t_bank")
+                for g in range(F_PASSES):
+                    nc.tensor.matmul_mx(
+                        out=t_banks[z][:],
+                        lhsT=w2_codes[:, j, g, :].bitcast(FP8X4),
+                        lhsT_scale=w2_scales[:, j, g, :],
+                        rhs=a_codes[:, n * F_PASSES + g, :].bitcast(FP8X4),
+                        rhs_scale=a_scales[:, n * F_PASSES + g, :],
+                        start=(g == 0),
+                        stop=(g == F_PASSES - 1),
+                    )
+
+            def add_residual(z):
+                n, j = divmod(z, D_TILES)
+                cols = slice(n * BLOCK, (n + 1) * BLOCK)
+                nc.vector.scalar_tensor_tensor(
+                    out=t_cols[:, j, cols],
+                    in0=t_banks[z][:],
+                    scalar=b2_col[:, j : j + 1],
+                    in1=h_grouped[:, cols, j],
+                    op0=ALU.add,
+                    op1=ALU.add,
+                    accum_out=sum_t[:, z : z + 1],
+                )
+
+            def square(z):
+                n, j = divmod(z, D_TILES)
+                squares = scratch.tile([P, BLOCK], BF16)
+                nc.scalar.activation(
+                    out=squares[:],
+                    in_=t_cols[:, j, n * BLOCK : (n + 1) * BLOCK],
+                    func=ACT.Square,
+                    accum_out=sum_sq[:, z : z + 1],
+                )
+
+            for z in range(-AHEAD, T_TILES):
+                if z + AHEAD < T_TILES:
+                    second_product(z + AHEAD)
+                if 0 <= z:
+                    add_residual(z)
+                    square(z)
+
             def transpose_back(q):
-                back_banks[q] = psum_back.tile([P, D_TILES, P], F32, tag="back", name="back_bank")
+                back_banks[q] = psum_ring.tile([P, D_TILES, P], F32, tag="ring", name="back_bank")
                 for j in range(D_TILES):
                     nc.tensor.transpose(
                         back_banks[q][:, j, :], t_cols[:, j, q * P : (q + 1) * P], ident[:]
                     )
 
-            for q in range(BACK_BANKS):
+            for q in range(RING):
                 transpose_back(q)
 
-            stat = small.tile([P, 2], F32)
+            stat = late.tile([P, 2], F32)
             nc.vector.tensor_reduce(out=stat[:, 0:1], in_=sum_t[:], axis=AXIS_X, op=ALU.add)
             nc.vector.tensor_reduce(out=stat[:, 1:2], in_=sum_sq[:], axis=AXIS_X, op=ALU.add)
             total = psum_tot.tile([P, 2], F32)
             nc.tensor.matmul(out=total[:], lhsT=ones[:], rhs=stat[:], start=True, stop=True)
-            moments = small.tile([P, 2], F32)
+            moments = late.tile([P, 2], F32)
             nc.vector.tensor_scalar(
                 out=moments[:], in0=total[:], scalar1=1.0 / (TOKENS * D), scalar2=None, op0=ALU.mult
             )
-            minus_var = small.tile([P, 1], F32)
+            minus_var = late.tile([P, 1], F32)
             nc.vector.scalar_tensor_tensor(
                 out=minus_var[:],
                 in0=moments[:, 0:1],
@@ -333,16 +327,16 @@ def tile_decoderblock_pb_t_kernel(tc, h2, w_ff1, b_ff1, w_ff2, b_ff2, out):
                 op0=ALU.mult,
                 op1=ALU.subtract,
             )
-            std = small.tile([P, 1], F32)
+            std = late.tile([P, 1], F32)
             nc.scalar.activation(out=std[:], in_=minus_var[:], func=ACT.Sqrt, scale=-1.0, bias=eps_col[:])
-            rstd = small.tile([P, 1], F32)
+            rstd = late.tile([P, 1], F32)
             nc.vector.reciprocal(out=rstd[:], in_=std[:])
-            shift = small.tile([P, 1], F32)
+            shift = late.tile([P, 1], F32)
             nc.vector.scalar_tensor_tensor(
                 out=shift[:], in0=moments[:, 0:1], scalar=-1.0, in1=rstd[:], op0=ALU.mult, op1=ALU.mult
             )
 
-            for q in range(TOKENS // P):
+            for q in range(N_PIECES):
                 n, s = divmod(q, SUB)
                 if s % 2 == 0:
                     o_rows = store.tile([P, 2, D], F32)
@@ -358,5 +352,5 @@ def tile_decoderblock_pb_t_kernel(tc, h2, w_ff1, b_ff1, w_ff2, b_ff2, out):
                         out=out_blocks[n][:, (s - 1) * D : (s + 1) * D],
                         in_=o_rows[:].rearrange("r s d -> r (s d)"),
                     )
-                if q + BACK_BANKS < TOKENS // P:
-                    transpose_back(q + BACK_BANKS)
+                if q + RING < N_PIECES:
+                    transpose_back(q + RING)

@@ -19,17 +19,22 @@ F = 1024
 TOKENS = 2 * 2048
 BLOCK = 512
 SUB = BLOCK // P
-SLAB = 2 * P
+UNIT = 2 * P
+CHUNK = 2048
 N_BLOCKS = TOKENS // BLOCK
-N_SLABS = TOKENS // SLAB
+N_SLABS = TOKENS // UNIT
 N_PIECES = TOKENS // P
 F_TILES = F // P
 D_TILES = D // P
 F_PASSES = F // (P * PACK)
+W_UNITS = 4
 ROUNDS = N_BLOCKS * F_PASSES
 T_TILES = N_BLOCKS * D_TILES
-RING = 7
+HEAD_SLABS = 4
+W2_FROM = 2
+EARLY_FROM = 6
 AHEAD = 4
+PREFILL = 7
 EPS = 1e-5
 
 FLOPS = 2 * TOKENS * D * F * 2
@@ -44,6 +49,22 @@ def tile_decoderblock_pb_t_kernel(tc, h2, w_ff1, b_ff1, w_ff2, b_ff2, out):
     with ExitStack() as whole:
         whole.enter_context(tc.manual_schedule())
         keep = whole.enter_context(tc.tile_pool(name="keep", bufs=1))
+        chunks = whole.enter_context(tc.tile_pool(name="chunks", bufs=8))
+        work = whole.enter_context(tc.tile_pool(name="work", bufs=2))
+        w_work = whole.enter_context(tc.tile_pool(name="w_work", bufs=4))
+        psum_x = whole.enter_context(tc.psum_pool(name="psum_x", bufs=4))
+        psum_a = whole.enter_context(tc.psum_pool(name="psum_a", bufs=4))
+
+        b1_bf = keep.tile([P, F_TILES], BF16)
+        nc.scalar.dma_start(
+            out=b1_bf[:].rearrange("m (c e) -> m c e", e=2),
+            in_=b_ff1.rearrange("(c m e) -> m c e", m=P, e=2),
+        )
+        b2_bf = keep.tile([P, D_TILES], BF16)
+        nc.scalar.dma_start(
+            out=b2_bf[:].rearrange("m (u e) -> m u e", e=2),
+            in_=b_ff2.rearrange("(u m e) -> m u e", m=P, e=2),
+        )
 
         ident = keep.tile([P, P], F32)
         make_identity(nc, ident[:])
@@ -59,298 +80,294 @@ def tile_decoderblock_pb_t_kernel(tc, h2, w_ff1, b_ff1, w_ff2, b_ff2, out):
         h_scales = keep.tile([P, TOKENS], U8, align_bytes=64)
         a_codes = keep.tile([P, ROUNDS, BLOCK], U32, align_bytes=64)
         a_scales = keep.tile([P, ROUNDS, BLOCK], U8, align_bytes=64)
-        w1_codes = keep.tile([P, F_TILES, P], U32, align_bytes=64)
-        w1_scales = keep.tile([P, F_TILES, P], U8, align_bytes=64)
-        w2_codes = keep.tile([P, D_TILES, F_PASSES, P], U32, align_bytes=64)
-        w2_scales = keep.tile([P, D_TILES, F_PASSES, P], U8, align_bytes=64)
+        w1_codes = keep.tile([P, F_TILES * P], U32, align_bytes=64)
+        w1_scales = keep.tile([P, F_TILES * P], U8, align_bytes=64)
+        w2_codes = keep.tile([P, D_TILES * F_PASSES * P], U32, align_bytes=64)
+        w2_scales = keep.tile([P, D_TILES * F_PASSES * P], U8, align_bytes=64)
         b1_col = keep.tile([P, F_TILES], F32)
         b2_col = keep.tile([P, D_TILES], F32)
         sum_t = keep.tile([P, T_TILES], F32)
         sum_sq = keep.tile([P, T_TILES], F32)
+        t_cols = keep.tile([P, D_TILES, TOKENS], F32)
 
         h_grouped_words = h_grouped[:].bitcast(F32)
 
-        with ExitStack() as first:
-            stage = first.enter_context(tc.tile_pool(name="stage", bufs=1))
-            work = first.enter_context(tc.tile_pool(name="work", bufs=2))
-            psum_x = first.enter_context(tc.psum_pool(name="psum_x", bufs=4))
-            psum_a = first.enter_context(tc.psum_pool(name="psum_a", bufs=PACK))
+        raw_words = {}
 
-            h_raw = stage.tile([P, N_SLABS, 2 * D], BF16)
-            w1_raw = stage.tile([P, F_TILES, D], BF16)
-            w2_raw = stage.tile([P, D_TILES, F], BF16)
+        def load(key, rows):
+            raw = chunks.tile([P, CHUNK], BF16, tag="chunk", name="raw")
+            nc.sync.dma_start(out=raw[:], in_=rows)
+            raw_words[key] = raw[:].bitcast(F32)
 
-            def load_h(n):
-                nc.sync.dma_start(
-                    out=h_raw[:, 2 * n : 2 * n + 2, :].rearrange("r y w -> r (y w)"), in_=h_blocks[n]
-                )
+        def load_h(n):
+            load(("h", n), h_blocks[n])
 
-            load_h(0)
-            for g in range(F_PASSES):
-                nc.sync.dma_start(
-                    out=w1_raw[:, g * PACK : (g + 1) * PACK, :].rearrange("m (u e) d -> m u (e d)", e=2),
-                    in_=w_ff1[g * P * PACK : (g + 1) * P * PACK, :].rearrange(
-                        "(u m e) d -> m u (e d)", m=P, e=2
-                    ),
-                )
-            for n in range(1, N_BLOCKS):
-                load_h(n)
+        def load_w1(g):
+            raw = chunks.tile([P, CHUNK], BF16, tag="chunk", name="raw")
             nc.sync.dma_start(
-                out=w2_raw[:].rearrange("m (u e) f -> m u (e f)", e=2),
-                in_=w_ff2.rearrange("(u m e) f -> m u (e f)", m=P, e=2),
+                out=raw[:].rearrange("m (u x) -> m u x", u=2),
+                in_=w_ff1[g * P * PACK : (g + 1) * P * PACK, :].rearrange("(u m e) d -> m u (e d)", m=P, e=2),
             )
-            b1_bf = stage.tile([P, F_TILES], BF16)
-            nc.scalar.dma_start(
-                out=b1_bf[:].rearrange("m (c e) -> m c e", e=2),
-                in_=b_ff1.rearrange("(c m e) -> m c e", m=P, e=2),
+            raw_words["w1", g] = raw[:].bitcast(F32)
+
+        def load_w2(u):
+            load(("w2", u), w_ff2[u * UNIT : (u + 1) * UNIT, :].rearrange("(m e) f -> m (e f)", e=2))
+
+        load_w1(0)
+        load_h(0)
+        load_w1(1)
+        for n in range(1, 4):
+            load_h(n)
+        load_w2(0)
+        load_w2(1)
+        for n in range(4, N_BLOCKS):
+            load_h(n)
+
+        x_banks = {}
+        w_grouped = {}
+        a_banks = {}
+        a_rows = {}
+        a_grouped = {}
+        t_banks = {}
+        back_banks = {}
+        ring_count = [0]
+
+        def ring_bank(shape, name):
+            ring_count[0] += 1
+            if ring_count[0] % 2 == 1:
+                return psum_x.tile(shape, F32, tag="x", name=name)
+            return psum_a.tile(shape, F32, tag="a", name=name)
+
+        def turn(kind, i):
+            words = raw_words[kind, i // 2][:, (i % 2) * 4 * P : (i % 2 + 1) * 4 * P]
+            x_banks[kind, i] = psum_x.tile([P, 4, P], F32, tag="x", name="x_bank")
+            for k in range(4):
+                nc.tensor.transpose(x_banks[kind, i][:, k, :], words[:, k * P : (k + 1) * P], ident[:])
+
+        def lay(kind, i, on_scalar):
+            if kind == "h":
+                grouped_words = h_grouped_words[:, i * UNIT : (i + 1) * UNIT, :]
+            else:
+                w_grouped[kind, i] = w_work.tile([P, UNIT, PACK], BF16, align_bytes=64, name="w_grouped")
+                grouped_words = w_grouped[kind, i][:].bitcast(F32)
+            dst = grouped_words.rearrange("p (a r) u -> p a r u", a=2)
+            src = x_banks[kind, i][:].rearrange("p (a u) r -> p a r u", u=2)
+            if on_scalar:
+                nc.scalar.copy(out=dst, in_=src)
+            else:
+                nc.vector.tensor_copy(out=dst, in_=src)
+
+        def quantise(kind, i):
+            cols = slice(i * UNIT, (i + 1) * UNIT)
+            if kind == "h":
+                codes, scales, grouped = h_codes, h_scales, h_grouped[:, cols, :]
+            elif kind == "w1":
+                codes, scales, grouped = w1_codes, w1_scales, w_grouped[kind, i][:]
+            else:
+                codes, scales, grouped = w2_codes, w2_scales, w_grouped[kind, i][:]
+            nc.vector.quantize_mx(
+                out=codes[:, cols].bitcast(FP8X4),
+                scales=scales[:, cols],
+                in_=grouped.rearrange("p c v -> p (c v)"),
             )
-            b2_bf = stage.tile([P, D_TILES], BF16)
-            nc.scalar.dma_start(
-                out=b2_bf[:].rearrange("m (u e) -> m u e", e=2),
-                in_=b_ff2.rearrange("(u m e) -> m u e", m=P, e=2),
+
+        def first_product(x, v):
+            n, g = divmod(x, F_PASSES)
+            cols = slice(n * BLOCK, (n + 1) * BLOCK)
+            rows = slice((g * PACK + v) * P, (g * PACK + v + 1) * P)
+            a_banks[x, v] = psum_a.tile([P, BLOCK], F32, tag="a", name="a_bank")
+            nc.tensor.matmul_mx(
+                out=a_banks[x, v][:],
+                lhsT=w1_codes[:, rows].bitcast(FP8X4),
+                lhsT_scale=w1_scales[:, rows],
+                rhs=h_codes[:, cols].bitcast(FP8X4),
+                rhs_scale=h_scales[:, cols],
+                start=True,
+                stop=True,
             )
 
-            h_words = h_raw[:].bitcast(F32)
-            w1_words = w1_raw[:].bitcast(F32)
-            w2_words = w2_raw[:].bitcast(F32)
-            w1_grouped = stage.tile([P, F_TILES, P, PACK], BF16, align_bytes=64)
-            w1_grouped_words = w1_grouped[:].bitcast(F32)
-            w2_grouped = stage.tile([P, D_TILES, F_PASSES, P, PACK], BF16, align_bytes=64)
-            w2_grouped_words = w2_grouped[:].bitcast(F32)
+        def relu_out(x, v):
+            if v == 0:
+                a_rows[x] = work.tile([P, PACK, BLOCK], BF16, name="a_rows")
+            i = (x % F_PASSES) * PACK + v
+            nc.scalar.activation(
+                out=a_rows[x][:, v, :], in_=a_banks[x, v][:], func=ACT.Relu, bias=b1_col[:, i : i + 1]
+            )
 
-            x_banks = {}
-            a_banks = {}
-            a_rows = {}
-            a_grouped = {}
+        def group_a(x):
+            a_grouped[x] = work.tile([P, BLOCK, PACK], BF16, align_bytes=64, name="a_grouped")
+            nc.vector.tensor_copy(
+                out=a_grouped[x][:].rearrange("p (c i) v -> p c v i", i=4),
+                in_=a_rows[x][:].rearrange("p v (c i) -> p c v i", i=4),
+            )
 
-            def transpose_words(key, words):
-                x_banks[key] = psum_x.tile([P, 4, P], F32, tag="x", name="x_bank")
-                for k in range(4):
-                    nc.tensor.transpose(x_banks[key][:, k, :], words[:, k * P : (k + 1) * P], ident[:])
+        def quantise_a(x):
+            nc.vector.quantize_mx(
+                out=a_codes[:, x, :].bitcast(FP8X4),
+                scales=a_scales[:, x, :],
+                in_=a_grouped[x][:].rearrange("p c v -> p (c v)"),
+            )
 
-            def transpose_h(y):
-                transpose_words(("h", y), h_words[:, y, :])
-
-            def group_h(y):
-                cols = slice(y * SLAB, (y + 1) * SLAB)
-                nc.vector.tensor_copy(
-                    out=h_grouped_words[:, cols, :].rearrange("p (s r) u -> p s r u", s=2),
-                    in_=x_banks["h", y][:].rearrange("p (s u) r -> p s r u", u=2),
-                )
-
-            def quantise_h(y):
-                cols = slice(y * SLAB, (y + 1) * SLAB)
-                nc.vector.quantize_mx(
-                    out=h_codes[:, cols].bitcast(FP8X4),
-                    scales=h_scales[:, cols],
-                    in_=h_grouped[:, cols, :].rearrange("p c v -> p (c v)"),
-                )
-
-            def pack_w1(g):
-                tiles = slice(g * PACK, (g + 1) * PACK)
-                for i in range(g * PACK, (g + 1) * PACK, 2):
-                    transpose_words(("w1", i), w1_words[:, i : i + 2, :].rearrange("m i w -> m (i w)"))
-                for i in range(g * PACK, (g + 1) * PACK, 2):
-                    nc.scalar.copy(
-                        out=w1_grouped_words[:, i : i + 2, :, :],
-                        in_=x_banks["w1", i][:].rearrange("p (i u) m -> p i m u", u=2),
-                    )
-                nc.vector.quantize_mx(
-                    out=w1_codes[:, tiles, :].rearrange("p i m -> p (i m)").bitcast(FP8X4),
-                    scales=w1_scales[:, tiles, :].rearrange("p i m -> p (i m)"),
-                    in_=w1_grouped[:, tiles, :, :].rearrange("p i m v -> p (i m v)"),
-                )
-
-            def pack_w2():
-                for j in range(D_TILES):
-                    transpose_words(("w2", j), w2_words[:, j, :])
-                for j in range(D_TILES):
-                    nc.scalar.copy(
-                        out=w2_grouped_words[:, j, :, :, :],
-                        in_=x_banks["w2", j][:].rearrange("p (g u) m -> p g m u", u=2),
-                    )
-                    nc.vector.quantize_mx(
-                        out=w2_codes[:, j, :, :].rearrange("p g m -> p (g m)").bitcast(FP8X4),
-                        scales=w2_scales[:, j, :, :].rearrange("p g m -> p (g m)"),
-                        in_=w2_grouped[:, j, :, :, :].rearrange("p g m v -> p (g m v)"),
-                    )
-
-            def first_product(x, v):
-                n, g = divmod(x, F_PASSES)
-                cols = slice(n * BLOCK, (n + 1) * BLOCK)
-                a_banks[x, v] = psum_a.tile([P, BLOCK], F32, tag="a", name="a_bank")
-                nc.tensor.matmul_mx(
-                    out=a_banks[x, v][:],
-                    lhsT=w1_codes[:, g * PACK + v, :].bitcast(FP8X4),
-                    lhsT_scale=w1_scales[:, g * PACK + v, :],
-                    rhs=h_codes[:, cols].bitcast(FP8X4),
-                    rhs_scale=h_scales[:, cols],
-                    start=True,
-                    stop=True,
-                )
-
-            def relu_out(x, v):
-                if v == 0:
-                    a_rows[x] = work.tile([P, PACK, BLOCK], BF16, name="a_rows")
-                i = (x % F_PASSES) * PACK + v
-                nc.scalar.activation(
-                    out=a_rows[x][:, v, :], in_=a_banks[x, v][:], func=ACT.Relu, bias=b1_col[:, i : i + 1]
-                )
-
-            def group_a(x):
-                a_grouped[x] = work.tile([P, BLOCK, PACK], BF16, align_bytes=64, name="a_grouped")
-                nc.vector.tensor_copy(
-                    out=a_grouped[x][:].rearrange("p (c i) v -> p c v i", i=4),
-                    in_=a_rows[x][:].rearrange("p v (c i) -> p c v i", i=4),
-                )
-
-            def quantise_a(x):
-                nc.vector.quantize_mx(
-                    out=a_codes[:, x, :].bitcast(FP8X4),
-                    scales=a_scales[:, x, :],
-                    in_=a_grouped[x][:].rearrange("p c v -> p (c v)"),
-                )
-
-            transpose_h(0)
-            transpose_h(1)
-            group_h(0)
-            group_h(1)
-            quantise_h(0)
-            quantise_h(1)
-            nc.vector.tensor_copy(out=b1_col[:], in_=b1_bf[:])
-            nc.vector.tensor_copy(out=b2_col[:], in_=b2_bf[:])
+        def second_product(z, early):
+            n, j = divmod(z, D_TILES)
+            if early:
+                t_banks[z] = psum_x.tile([P, BLOCK], F32, tag="x", name="t_bank")
+            else:
+                t_banks[z] = ring_bank([P, BLOCK], "t_bank")
             for g in range(F_PASSES):
-                pack_w1(g)
+                rows = slice((j * F_PASSES + g) * P, (j * F_PASSES + g + 1) * P)
+                nc.tensor.matmul_mx(
+                    out=t_banks[z][:],
+                    lhsT=w2_codes[:, rows].bitcast(FP8X4),
+                    lhsT_scale=w2_scales[:, rows],
+                    rhs=a_codes[:, n * F_PASSES + g, :].bitcast(FP8X4),
+                    rhs_scale=a_scales[:, n * F_PASSES + g, :],
+                    start=(g == 0),
+                    stop=(g == F_PASSES - 1),
+                )
+
+        def add_residual(z):
+            n, j = divmod(z, D_TILES)
+            cols = slice(n * BLOCK, (n + 1) * BLOCK)
+            nc.vector.scalar_tensor_tensor(
+                out=t_cols[:, j, cols],
+                in0=t_banks[z][:],
+                scalar=b2_col[:, j : j + 1],
+                in1=h_grouped[:, cols, j],
+                op0=ALU.add,
+                op1=ALU.add,
+                accum_out=sum_t[:, z : z + 1],
+            )
+
+        def square(z):
+            n, j = divmod(z, D_TILES)
+            squares = work.tile([P, BLOCK], BF16, name="squares")
+            nc.scalar.activation(
+                out=squares[:],
+                in_=t_cols[:, j, n * BLOCK : (n + 1) * BLOCK],
+                func=ACT.Square,
+                accum_out=sum_sq[:, z : z + 1],
+            )
+
+        def transpose_back(q):
+            back_banks[q] = ring_bank([P, D_TILES, P], "back_bank")
+            for j in range(D_TILES):
+                nc.tensor.transpose(back_banks[q][:, j, :], t_cols[:, j, q * P : (q + 1) * P], ident[:])
+
+        nc.vector.tensor_copy(out=b1_col[:], in_=b1_bf[:])
+        nc.vector.tensor_copy(out=b2_col[:], in_=b2_bf[:])
+        turn("w1", 0)
+        turn("w1", 1)
+        lay("w1", 0, True)
+        lay("w1", 1, False)
+        turn("h", 0)
+        turn("h", 1)
+        quantise("w1", 0)
+        lay("h", 0, True)
+        lay("h", 1, False)
+        quantise("w1", 1)
+        quantise("h", 0)
+        turn("w1", 2)
+        turn("w1", 3)
+        quantise("h", 1)
+        for v in range(PACK):
+            first_product(0, v)
+        lay("w1", 2, True)
+        lay("w1", 3, True)
+        turn("h", 2)
+        turn("h", 3)
+        quantise("w1", 2)
+        quantise("w1", 3)
+        lay("h", 2, False)
+        lay("h", 3, False)
+        turn("h", 4)
+        quantise("h", 2)
+        quantise("h", 3)
+
+        for x in range(ROUNDS):
+            if 0 <= x - 1:
+                quantise_a(x - 1)
+            if HEAD_SLABS <= x + 3 < N_SLABS:
+                quantise("h", x + 3)
             for v in range(PACK):
-                first_product(0, v)
+                relu_out(x, v)
+                if x + 1 < ROUNDS:
+                    first_product(x + 1, v)
+            if x + 5 < N_SLABS:
+                turn("h", x + 5)
+            if x + 4 < N_SLABS:
+                lay("h", x + 4, True)
+            if 0 <= x - W2_FROM < W_UNITS:
+                turn("w2", x - W2_FROM)
+            group_a(x)
+            if 0 <= x - W2_FROM < W_UNITS:
+                lay("w2", x - W2_FROM, False)
+            if 0 <= x - W2_FROM - 1 < W_UNITS:
+                quantise("w2", x - W2_FROM - 1)
+            if EARLY_FROM <= x:
+                second_product(x - EARLY_FROM, True)
+            if EARLY_FROM <= x - 1:
+                add_residual(x - 1 - EARLY_FROM)
 
-            for x in range(-3, ROUNDS):
-                if 0 <= x - 1:
-                    quantise_a(x - 1)
-                if 2 <= x + 3 < N_SLABS:
-                    quantise_h(x + 3)
-                for v in range(PACK):
-                    if 0 <= x:
-                        relu_out(x, v)
-                    if 1 <= x + 1 < ROUNDS:
-                        first_product(x + 1, v)
-                if 2 <= x + 5 < N_SLABS:
-                    transpose_h(x + 5)
-                if 0 <= x:
-                    group_a(x)
-                if 2 <= x + 4 < N_SLABS:
-                    group_h(x + 4)
+        n_early = ROUNDS - EARLY_FROM
+        add_residual(n_early - 1)
+        for z in range(n_early):
+            square(z)
+        for z in range(n_early, n_early + AHEAD):
+            second_product(z, False)
+        for z in range(n_early, T_TILES):
+            add_residual(z)
+            if z == n_early:
+                quantise_a(ROUNDS - 1)
+            if z + AHEAD < T_TILES:
+                second_product(z + AHEAD, False)
+            square(z)
 
-            pack_w2()
-            quantise_a(ROUNDS - 1)
+        for q in range(PREFILL):
+            transpose_back(q)
 
-        with ExitStack() as rest:
-            late = rest.enter_context(tc.tile_pool(name="late", bufs=1))
-            scratch = rest.enter_context(tc.tile_pool(name="scratch", bufs=2))
-            store = rest.enter_context(tc.tile_pool(name="store", bufs=6))
-            psum_tot = rest.enter_context(tc.psum_pool(name="psum_tot", bufs=1, reuse_waits="tile"))
-            psum_ring = rest.enter_context(tc.psum_pool(name="psum_ring", bufs=RING, reuse_waits="tile"))
+        stat = keep.tile([P, 2], F32)
+        nc.vector.tensor_reduce(out=stat[:, 0:1], in_=sum_t[:], axis=AXIS_X, op=ALU.add)
+        nc.vector.tensor_reduce(out=stat[:, 1:2], in_=sum_sq[:], axis=AXIS_X, op=ALU.add)
+        total = ring_bank([P, 2], "total")
+        nc.tensor.matmul(out=total[:], lhsT=ones[:], rhs=stat[:], start=True, stop=True)
+        moments = keep.tile([P, 2], F32)
+        nc.vector.tensor_scalar(
+            out=moments[:], in0=total[:], scalar1=1.0 / (TOKENS * D), scalar2=None, op0=ALU.mult
+        )
+        minus_var = keep.tile([P, 1], F32)
+        nc.vector.scalar_tensor_tensor(
+            out=minus_var[:],
+            in0=moments[:, 0:1],
+            scalar=moments[:, 0:1],
+            in1=moments[:, 1:2],
+            op0=ALU.mult,
+            op1=ALU.subtract,
+        )
+        std = keep.tile([P, 1], F32)
+        nc.scalar.activation(out=std[:], in_=minus_var[:], func=ACT.Sqrt, scale=-1.0, bias=eps_col[:])
+        rstd = keep.tile([P, 1], F32)
+        nc.vector.reciprocal(out=rstd[:], in_=std[:])
+        shift = keep.tile([P, 1], F32)
+        nc.vector.scalar_tensor_tensor(
+            out=shift[:], in0=moments[:, 0:1], scalar=-1.0, in1=rstd[:], op0=ALU.mult, op1=ALU.mult
+        )
 
-            t_cols = late.tile([P, D_TILES, TOKENS], F32)
-            t_banks = {}
-            back_banks = {}
-
-            def second_product(z):
-                n, j = divmod(z, D_TILES)
-                t_banks[z] = psum_ring.tile([P, BLOCK], F32, tag="ring", name="t_bank")
-                for g in range(F_PASSES):
-                    nc.tensor.matmul_mx(
-                        out=t_banks[z][:],
-                        lhsT=w2_codes[:, j, g, :].bitcast(FP8X4),
-                        lhsT_scale=w2_scales[:, j, g, :],
-                        rhs=a_codes[:, n * F_PASSES + g, :].bitcast(FP8X4),
-                        rhs_scale=a_scales[:, n * F_PASSES + g, :],
-                        start=(g == 0),
-                        stop=(g == F_PASSES - 1),
-                    )
-
-            def add_residual(z):
-                n, j = divmod(z, D_TILES)
-                cols = slice(n * BLOCK, (n + 1) * BLOCK)
-                nc.vector.scalar_tensor_tensor(
-                    out=t_cols[:, j, cols],
-                    in0=t_banks[z][:],
-                    scalar=b2_col[:, j : j + 1],
-                    in1=h_grouped[:, cols, j],
-                    op0=ALU.add,
-                    op1=ALU.add,
-                    accum_out=sum_t[:, z : z + 1],
+        for q in range(N_PIECES):
+            n, s = divmod(q, SUB)
+            if s % 2 == 0:
+                o_rows = chunks.tile([P, 2, D], F32, tag="chunk", name="o_rows")
+            src = back_banks[q][:].rearrange("r (u e) m -> r u m e", e=2)
+            dst = o_rows[:, s % 2, :].rearrange("r (u m e) -> r u m e", u=2, e=2)
+            if s % 2 == 0:
+                nc.scalar.activation(out=dst, in_=src, func=ACT.Identity, scale=rstd[:], bias=shift[:])
+            else:
+                nc.vector.tensor_scalar(
+                    out=dst, in0=src, scalar1=rstd[:], scalar2=shift[:], op0=ALU.mult, op1=ALU.add
                 )
-
-            def square(z):
-                n, j = divmod(z, D_TILES)
-                squares = scratch.tile([P, BLOCK], BF16)
-                nc.scalar.activation(
-                    out=squares[:],
-                    in_=t_cols[:, j, n * BLOCK : (n + 1) * BLOCK],
-                    func=ACT.Square,
-                    accum_out=sum_sq[:, z : z + 1],
+                nc.sync.dma_start(
+                    out=out_blocks[n][:, (s - 1) * D : (s + 1) * D],
+                    in_=o_rows[:].rearrange("r s d -> r (s d)"),
                 )
-
-            for z in range(-AHEAD, T_TILES):
-                if z + AHEAD < T_TILES:
-                    second_product(z + AHEAD)
-                if 0 <= z:
-                    add_residual(z)
-                    square(z)
-
-            def transpose_back(q):
-                back_banks[q] = psum_ring.tile([P, D_TILES, P], F32, tag="ring", name="back_bank")
-                for j in range(D_TILES):
-                    nc.tensor.transpose(
-                        back_banks[q][:, j, :], t_cols[:, j, q * P : (q + 1) * P], ident[:]
-                    )
-
-            for q in range(RING):
-                transpose_back(q)
-
-            stat = late.tile([P, 2], F32)
-            nc.vector.tensor_reduce(out=stat[:, 0:1], in_=sum_t[:], axis=AXIS_X, op=ALU.add)
-            nc.vector.tensor_reduce(out=stat[:, 1:2], in_=sum_sq[:], axis=AXIS_X, op=ALU.add)
-            total = psum_tot.tile([P, 2], F32)
-            nc.tensor.matmul(out=total[:], lhsT=ones[:], rhs=stat[:], start=True, stop=True)
-            moments = late.tile([P, 2], F32)
-            nc.vector.tensor_scalar(
-                out=moments[:], in0=total[:], scalar1=1.0 / (TOKENS * D), scalar2=None, op0=ALU.mult
-            )
-            minus_var = late.tile([P, 1], F32)
-            nc.vector.scalar_tensor_tensor(
-                out=minus_var[:],
-                in0=moments[:, 0:1],
-                scalar=moments[:, 0:1],
-                in1=moments[:, 1:2],
-                op0=ALU.mult,
-                op1=ALU.subtract,
-            )
-            std = late.tile([P, 1], F32)
-            nc.scalar.activation(out=std[:], in_=minus_var[:], func=ACT.Sqrt, scale=-1.0, bias=eps_col[:])
-            rstd = late.tile([P, 1], F32)
-            nc.vector.reciprocal(out=rstd[:], in_=std[:])
-            shift = late.tile([P, 1], F32)
-            nc.vector.scalar_tensor_tensor(
-                out=shift[:], in0=moments[:, 0:1], scalar=-1.0, in1=rstd[:], op0=ALU.mult, op1=ALU.mult
-            )
-
-            for q in range(N_PIECES):
-                n, s = divmod(q, SUB)
-                if s % 2 == 0:
-                    o_rows = store.tile([P, 2, D], F32)
-                src = back_banks[q][:].rearrange("r (u e) m -> r u m e", e=2)
-                dst = o_rows[:, s % 2, :].rearrange("r (u m e) -> r u m e", u=2, e=2)
-                if s % 2 == 0:
-                    nc.scalar.activation(out=dst, in_=src, func=ACT.Identity, scale=rstd[:], bias=shift[:])
-                else:
-                    nc.vector.tensor_scalar(
-                        out=dst, in0=src, scalar1=rstd[:], scalar2=shift[:], op0=ALU.mult, op1=ALU.add
-                    )
-                    nc.sync.dma_start(
-                        out=out_blocks[n][:, (s - 1) * D : (s + 1) * D],
-                        in_=o_rows[:].rearrange("r s d -> r (s d)"),
-                    )
-                if q + RING < N_PIECES:
-                    transpose_back(q + RING)
+            if q + PREFILL < N_PIECES:
+                transpose_back(q + PREFILL)

@@ -68,8 +68,8 @@ def tile_decoderblock_pb_t_kernel(tc, h2, w_ff1, b_ff1, w_ff2, b_ff2, out):
 
         ident = keep.tile([P, P], F32)
         make_identity(nc, ident[:])
-        ones = keep.tile([P, P], F32)
-        nc.vector.memset(ones[:], 1.0)
+        averager = keep.tile([P, P], F32)
+        nc.vector.memset(averager[:], 1.0 / (TOKENS * D))
         eps_col = keep.tile([P, 1], F32)
         nc.vector.memset(eps_col[:], EPS)
         table_warm = keep.tile([P, 1], F32)
@@ -86,8 +86,7 @@ def tile_decoderblock_pb_t_kernel(tc, h2, w_ff1, b_ff1, w_ff2, b_ff2, out):
         w2_scales = keep.tile([P, D_TILES * F_PASSES * P], U8, align_bytes=64)
         b1_col = keep.tile([P, F_TILES], F32)
         b2_col = keep.tile([P, D_TILES], F32)
-        sum_t = keep.tile([P, T_TILES], F32)
-        sum_sq = keep.tile([P, T_TILES], F32)
+        sums = keep.tile([P, T_TILES, 2], F32)
         t_cols = keep.tile([P, D_TILES, TOKENS], F32)
 
         h_grouped_words = h_grouped[:].bitcast(F32)
@@ -236,7 +235,7 @@ def tile_decoderblock_pb_t_kernel(tc, h2, w_ff1, b_ff1, w_ff2, b_ff2, out):
                 in1=h_grouped[:, cols, j],
                 op0=ALU.add,
                 op1=ALU.add,
-                accum_out=sum_t[:, z : z + 1],
+                accum_out=sums[:, z, 0:1],
             )
 
         def square(z):
@@ -246,7 +245,7 @@ def tile_decoderblock_pb_t_kernel(tc, h2, w_ff1, b_ff1, w_ff2, b_ff2, out):
                 out=squares[:],
                 in_=t_cols[:, j, n * BLOCK : (n + 1) * BLOCK],
                 func=ACT.Square,
-                accum_out=sum_sq[:, z : z + 1],
+                accum_out=sums[:, z, 1:2],
             )
 
         def transpose_back(q):
@@ -327,31 +326,29 @@ def tile_decoderblock_pb_t_kernel(tc, h2, w_ff1, b_ff1, w_ff2, b_ff2, out):
             transpose_back(q)
 
         stat = keep.tile([P, 2], F32)
-        nc.vector.tensor_reduce(out=stat[:, 0:1], in_=sum_t[:], axis=AXIS_X, op=ALU.add)
-        nc.vector.tensor_reduce(out=stat[:, 1:2], in_=sum_sq[:], axis=AXIS_X, op=ALU.add)
-        total = ring_bank([P, 2], "total")
-        nc.tensor.matmul(out=total[:], lhsT=ones[:], rhs=stat[:], start=True, stop=True)
-        moments = keep.tile([P, 2], F32)
-        nc.vector.tensor_scalar(
-            out=moments[:], in0=total[:], scalar1=1.0 / (TOKENS * D), scalar2=None, op0=ALU.mult
+        nc.vector.tensor_reduce(
+            out=stat[:], in_=sums[:, 0 : T_TILES - 1, :].rearrange("p z c -> p c z"), axis=AXIS_X, op=ALU.add
         )
+        moments = ring_bank([P, 2], "moments")
+        nc.tensor.matmul(out=moments[:], lhsT=averager[:], rhs=stat[:], start=True, stop=False)
+        nc.tensor.matmul(out=moments[:], lhsT=averager[:], rhs=sums[:, T_TILES - 1, :], start=False, stop=True)
         minus_var = keep.tile([P, 1], F32)
-        nc.vector.scalar_tensor_tensor(
+        nc.vector.tensor_scalar(
             out=minus_var[:],
             in0=moments[:, 0:1],
-            scalar=moments[:, 0:1],
-            in1=moments[:, 1:2],
+            scalar1=moments[:, 0:1],
+            scalar2=moments[:, 1:2],
             op0=ALU.mult,
             op1=ALU.subtract,
         )
         std = keep.tile([P, 1], F32)
         nc.scalar.activation(out=std[:], in_=minus_var[:], func=ACT.Sqrt, scale=-1.0, bias=eps_col[:])
+        minus_mean = keep.tile([P, 1], F32)
+        nc.vector.tensor_scalar(out=minus_mean[:], in0=moments[:, 0:1], scalar1=-1.0, scalar2=None, op0=ALU.mult)
         rstd = keep.tile([P, 1], F32)
         nc.vector.reciprocal(out=rstd[:], in_=std[:])
         shift = keep.tile([P, 1], F32)
-        nc.vector.scalar_tensor_tensor(
-            out=shift[:], in0=moments[:, 0:1], scalar=-1.0, in1=rstd[:], op0=ALU.mult, op1=ALU.mult
-        )
+        nc.scalar.activation(out=shift[:], in_=minus_mean[:], func=ACT.Identity, scale=rstd[:])
 
         for q in range(N_PIECES):
             n, s = divmod(q, SUB)
@@ -363,7 +360,7 @@ def tile_decoderblock_pb_t_kernel(tc, h2, w_ff1, b_ff1, w_ff2, b_ff2, out):
                 nc.scalar.activation(out=dst, in_=src, func=ACT.Identity, scale=rstd[:], bias=shift[:])
             else:
                 nc.vector.tensor_scalar(
-                    out=dst, in0=src, scalar1=rstd[:], scalar2=shift[:], op0=ALU.mult, op1=ALU.add
+                    out=dst, in0=src, scalar1=minus_mean[:], scalar2=rstd[:], op0=ALU.add, op1=ALU.mult
                 )
                 nc.sync.dma_start(
                     out=out_blocks[n][:, (s - 1) * D : (s + 1) * D],

@@ -91,36 +91,49 @@ def tile_decoderblock_pb_t_kernel(tc, h2, w_ff1, b_ff1, w_ff2, b_ff2, out):
 
         h_grouped_words = h_grouped[:].bitcast(F32)
 
+        raw_tiles = {}
         raw_words = {}
 
-        def load(key, rows):
-            raw = chunks.tile([P, CHUNK], BF16, tag="chunk", name="raw")
-            nc.sync.dma_start(out=raw[:], in_=rows)
-            raw_words[key] = raw[:].bitcast(F32)
+        def rows_of(kind, c):
+            if kind == "h":
+                return h_blocks[c]
+            if kind == "w1":
+                return w_ff1[c * 2 * UNIT : (c + 1) * 2 * UNIT, :].rearrange("(u m e) d -> m u (e d)", m=P, e=2)
+            return w_ff2[c * UNIT : (c + 1) * UNIT, :].rearrange("(m e) f -> m (e f)", e=2)
 
-        def load_h(n):
-            load(("h", n), h_blocks[n])
+        def chunk_tile(kind, c):
+            if (kind, c) not in raw_tiles:
+                raw_tiles[kind, c] = chunks.tile([P, CHUNK], BF16, tag="chunk", name="raw")
+                raw_words[kind, c] = raw_tiles[kind, c][:].bitcast(F32)
+            return raw_tiles[kind, c]
 
-        def load_w1(g):
-            raw = chunks.tile([P, CHUNK], BF16, tag="chunk", name="raw")
-            nc.sync.dma_start(
-                out=raw[:].rearrange("m (u x) -> m u x", u=2),
-                in_=w_ff1[g * P * PACK : (g + 1) * P * PACK, :].rearrange("(u m e) d -> m u (e d)", m=P, e=2),
-            )
-            raw_words["w1", g] = raw[:].bitcast(F32)
+        def load_chunk(kind, c):
+            dst = chunk_tile(kind, c)[:]
+            if kind == "w1":
+                dst = dst.rearrange("m (u x) -> m u x", u=2)
+            nc.sync.dma_start(out=dst, in_=rows_of(kind, c))
 
-        def load_w2(u):
-            load(("w2", u), w_ff2[u * UNIT : (u + 1) * UNIT, :].rearrange("(m e) f -> m (e f)", e=2))
+        def load_unit(kind, i):
+            half = slice((i % 2) * (CHUNK // 2), (i % 2 + 1) * (CHUNK // 2))
+            if kind == "w1":
+                rows = rows_of(kind, i // 2)[:, i % 2, :]
+            else:
+                rows = rows_of(kind, i // 2)[:, half]
+            nc.sync.dma_start(out=chunk_tile(kind, i // 2)[:, half], in_=rows)
 
-        load_w1(0)
-        load_h(0)
-        load_w1(1)
-        for n in range(1, 4):
-            load_h(n)
-        load_w2(0)
-        load_w2(1)
+        load_unit("w1", 0)
+        load_unit("h", 0)
+        load_unit("h", 1)
+        for i in range(1, W_UNITS):
+            load_unit("w1", i)
+        load_unit("h", 2)
+        load_unit("h", 3)
+        load_chunk("h", 2)
+        load_chunk("h", 3)
+        load_chunk("w2", 0)
+        load_chunk("w2", 1)
         for n in range(4, N_BLOCKS):
-            load_h(n)
+            load_chunk("h", n)
 
         x_banks = {}
         w_grouped = {}
@@ -256,23 +269,25 @@ def tile_decoderblock_pb_t_kernel(tc, h2, w_ff1, b_ff1, w_ff2, b_ff2, out):
         nc.vector.tensor_copy(out=b1_col[:], in_=b1_bf[:])
         nc.vector.tensor_copy(out=b2_col[:], in_=b2_bf[:])
         turn("w1", 0)
-        turn("w1", 1)
         lay("w1", 0, True)
-        lay("w1", 1, False)
         turn("h", 0)
+        lay("h", 0, False)
         turn("h", 1)
         quantise("w1", 0)
-        lay("h", 0, True)
-        lay("h", 1, False)
-        quantise("w1", 1)
+        lay("h", 1, True)
+        turn("w1", 1)
         quantise("h", 0)
+        lay("w1", 1, True)
+        quantise("h", 1)
         turn("w1", 2)
         turn("w1", 3)
-        quantise("h", 1)
-        for v in range(PACK):
-            first_product(0, v)
+        first_product(0, 0)
+        first_product(0, 1)
+        quantise("w1", 1)
+        first_product(0, 2)
+        first_product(0, 3)
         lay("w1", 2, True)
-        lay("w1", 3, True)
+        lay("w1", 3, False)
         turn("h", 2)
         turn("h", 3)
         quantise("w1", 2)

@@ -32,7 +32,7 @@ ROUNDS = N_BLOCKS * F_PASSES
 T_TILES = N_BLOCKS * D_TILES
 HEAD_SLABS = 4
 W2_FROM = 2
-EARLY_FROM = 6
+POOL_FROM = 10
 AHEAD = 4
 PREFILL = 7
 EPS = 1e-5
@@ -198,20 +198,40 @@ def tile_decoderblock_pb_t_kernel(tc, h2, w_ff1, b_ff1, w_ff2, b_ff2, out):
                 stop=True,
             )
 
-        def relu_out(x, v):
+        def relu_out(x, v, on_scalar):
             if v == 0:
-                a_rows[x] = work.tile([P, PACK, BLOCK], BF16, name="a_rows")
+                a_rows[x] = work.tile([P, PACK, BLOCK], BF16, name="a_rows", bufs=3)
             i = (x % F_PASSES) * PACK + v
-            nc.scalar.activation(
-                out=a_rows[x][:, v, :], in_=a_banks[x, v][:], func=ACT.Relu, bias=b1_col[:, i : i + 1]
-            )
+            if on_scalar:
+                nc.scalar.activation(
+                    out=a_rows[x][:, v, :], in_=a_banks[x, v][:], func=ACT.Relu, bias=b1_col[:, i : i + 1]
+                )
+            else:
+                nc.vector.tensor_scalar(
+                    out=a_rows[x][:, v, :],
+                    in0=a_banks[x, v][:],
+                    scalar1=b1_col[:, i : i + 1],
+                    scalar2=0.0,
+                    op0=ALU.add,
+                    op1=ALU.max,
+                )
 
-        def group_a(x):
-            a_grouped[x] = work.tile([P, BLOCK, PACK], BF16, align_bytes=64, name="a_grouped")
-            nc.vector.tensor_copy(
-                out=a_grouped[x][:].rearrange("p (c i) v -> p c v i", i=4),
-                in_=a_rows[x][:].rearrange("p v (c i) -> p c v i", i=4),
-            )
+        def group_a(x, on_vector):
+            a_grouped[x] = work.tile([P, BLOCK, PACK], BF16, align_bytes=64, name="a_grouped", bufs=1)
+            if on_vector:
+                nc.vector.tensor_copy(
+                    out=a_grouped[x][:].rearrange("p (c i) v -> p c v i", i=4),
+                    in_=a_rows[x][:].rearrange("p v (c i) -> p c v i", i=4),
+                )
+            else:
+                nc.gpsimd.tensor_scalar(
+                    out=a_grouped[x][:],
+                    in0=a_rows[x][:].rearrange("p v c -> p c v"),
+                    scalar1=1.0,
+                    scalar2=0.0,
+                    op0=ALU.mult,
+                    op1=ALU.add,
+                )
 
         def quantise_a(x):
             nc.vector.quantize_mx(
@@ -298,34 +318,57 @@ def tile_decoderblock_pb_t_kernel(tc, h2, w_ff1, b_ff1, w_ff2, b_ff2, out):
         quantise("h", 2)
         quantise("h", 3)
 
-        for x in range(ROUNDS):
+        for x in range(POOL_FROM):
             if 0 <= x - 1:
                 quantise_a(x - 1)
             if HEAD_SLABS <= x + 3 < N_SLABS:
                 quantise("h", x + 3)
             for v in range(PACK):
-                relu_out(x, v)
-                if x + 1 < ROUNDS:
-                    first_product(x + 1, v)
-            if x + 5 < N_SLABS:
-                turn("h", x + 5)
-            if x + 4 < N_SLABS:
-                lay("h", x + 4, True)
+                relu_out(x, v, True)
+                first_product(x + 1, v)
+            turn("h", x + 5)
+            lay("h", x + 4, True)
             if 0 <= x - W2_FROM < W_UNITS:
                 turn("w2", x - W2_FROM)
-            group_a(x)
+            group_a(x, True)
             if 0 <= x - W2_FROM < W_UNITS:
                 lay("w2", x - W2_FROM, False)
             if 0 <= x - W2_FROM - 1 < W_UNITS:
                 quantise("w2", x - W2_FROM - 1)
-            if EARLY_FROM <= x:
-                second_product(x - EARLY_FROM, True)
-            if EARLY_FROM <= x - 1:
-                add_residual(x - 1 - EARLY_FROM)
 
-        n_early = ROUNDS - EARLY_FROM
-        add_residual(n_early - 1)
-        for z in range(n_early):
+        for z in range(D_TILES):
+            second_product(z, True)
+        for v in range(PACK):
+            relu_out(POOL_FROM, v, True)
+            first_product(POOL_FROM + 1, v)
+        for x in range(POOL_FROM, ROUNDS):
+            z0 = (x - POOL_FROM) * D_TILES
+            if x + 3 < N_SLABS:
+                quantise("h", x + 3)
+            quantise_a(x - 1)
+            group_a(x, False)
+            if x + 5 < N_SLABS:
+                turn("h", x + 5)
+            for v in range(PACK - 1):
+                if x + 1 < ROUNDS:
+                    relu_out(x + 1, v, True)
+                if x + 2 < ROUNDS:
+                    first_product(x + 2, v)
+            if x + 4 < N_SLABS:
+                lay("h", x + 4, False)
+            for z in range(max(z0 - D_TILES, 0), z0):
+                square(z)
+            for z in range(z0, z0 + D_TILES):
+                add_residual(z)
+                if z + D_TILES < (ROUNDS - POOL_FROM) * D_TILES:
+                    second_product(z + D_TILES, True)
+            if x + 1 < ROUNDS:
+                relu_out(x + 1, PACK - 1, False)
+            if x + 2 < ROUNDS:
+                first_product(x + 2, PACK - 1)
+
+        n_early = (ROUNDS - POOL_FROM) * D_TILES
+        for z in range(n_early - D_TILES, n_early):
             square(z)
         for z in range(n_early, n_early + AHEAD):
             second_product(z, False)

@@ -34,7 +34,7 @@ HEAD_SLABS = 4
 W2_FROM = 2
 POOL_FROM = 10
 AHEAD = 4
-PREFILL = 7
+PREFILL = 6
 EPS = 1e-5
 
 FLOPS = 2 * TOKENS * D * F * 2
@@ -47,7 +47,8 @@ def tile_decoderblock_pb_t_kernel(tc, h2, w_ff1, b_ff1, w_ff2, b_ff2, out):
     out_blocks = out.flatten_outer_dims().rearrange("(n r s) d -> n r (s d)", r=P, s=SUB)
 
     with ExitStack() as whole:
-        whole.enter_context(tc.manual_schedule())
+        pinned = {mybir.EngineType.DVE, mybir.EngineType.Activation, mybir.EngineType.Pool, mybir.EngineType.SP}
+        whole.enter_context(tc.manual_schedule(engines=pinned))
         keep = whole.enter_context(tc.tile_pool(name="keep", bufs=1))
         chunks = whole.enter_context(tc.tile_pool(name="chunks", bufs=8))
         work = whole.enter_context(tc.tile_pool(name="work", bufs=2))
@@ -70,10 +71,10 @@ def tile_decoderblock_pb_t_kernel(tc, h2, w_ff1, b_ff1, w_ff2, b_ff2, out):
         make_identity(nc, ident[:])
         averager = keep.tile([P, P], F32)
         nc.vector.memset(averager[:], 1.0 / (TOKENS * D))
-        eps_col = keep.tile([P, 1], F32)
-        nc.vector.memset(eps_col[:], EPS)
+        warm_in = keep.tile([P, 1], F32)
+        nc.vector.memset(warm_in[:], 1.0)
         table_warm = keep.tile([P, 1], F32)
-        nc.scalar.activation(out=table_warm[:], in_=eps_col[:], func=ACT.Sqrt)
+        nc.scalar.activation(out=table_warm[:], in_=warm_in[:], func=ACT.Abs_reciprocal_sqrt)
 
         h_grouped = keep.tile([P, TOKENS, PACK], BF16, align_bytes=64)
         h_codes = keep.tile([P, TOKENS], U32, align_bytes=64)
@@ -384,27 +385,24 @@ def tile_decoderblock_pb_t_kernel(tc, h2, w_ff1, b_ff1, w_ff2, b_ff2, out):
             transpose_back(q)
 
         stat = keep.tile([P, 2], F32)
-        nc.vector.tensor_reduce(
-            out=stat[:], in_=sums[:, 0 : T_TILES - 1, :].rearrange("p z c -> p c z"), axis=AXIS_X, op=ALU.add
+        nc.vector.tensor_reduce(out=stat[:, 0:1], in_=sums[:, 0 : T_TILES - 1, 0], axis=AXIS_X, op=ALU.add)
+        mean = ring_bank([P, 1], "mean")
+        nc.tensor.matmul(out=mean[:], lhsT=averager[:], rhs=stat[:, 0:1], start=True, stop=False)
+        nc.tensor.matmul(out=mean[:], lhsT=averager[:], rhs=sums[:, T_TILES - 1, 0:1], start=False, stop=True)
+        nc.vector.tensor_reduce(out=stat[:, 1:2], in_=sums[:, 0 : T_TILES - 1, 1], axis=AXIS_X, op=ALU.add)
+        mean_square = ring_bank([P, 1], "mean_square")
+        nc.tensor.matmul(out=mean_square[:], lhsT=averager[:], rhs=stat[:, 1:2], start=True, stop=False)
+        nc.tensor.matmul(
+            out=mean_square[:], lhsT=averager[:], rhs=sums[:, T_TILES - 1, 1:2], start=False, stop=True
         )
-        moments = ring_bank([P, 2], "moments")
-        nc.tensor.matmul(out=moments[:], lhsT=averager[:], rhs=stat[:], start=True, stop=False)
-        nc.tensor.matmul(out=moments[:], lhsT=averager[:], rhs=sums[:, T_TILES - 1, :], start=False, stop=True)
-        minus_var = keep.tile([P, 1], F32)
-        nc.vector.tensor_scalar(
-            out=minus_var[:],
-            in0=moments[:, 0:1],
-            scalar1=moments[:, 0:1],
-            scalar2=moments[:, 1:2],
-            op0=ALU.mult,
-            op1=ALU.subtract,
-        )
-        std = keep.tile([P, 1], F32)
-        nc.scalar.activation(out=std[:], in_=minus_var[:], func=ACT.Sqrt, scale=-1.0, bias=eps_col[:])
         minus_mean = keep.tile([P, 1], F32)
-        nc.vector.tensor_scalar(out=minus_mean[:], in0=moments[:, 0:1], scalar1=-1.0, scalar2=None, op0=ALU.mult)
+        nc.vector.tensor_scalar(out=minus_mean[:], in0=mean[:], scalar1=-1.0, scalar2=None, op0=ALU.mult)
+        eps_minus = keep.tile([P, 1], F32)
+        nc.vector.tensor_scalar(
+            out=eps_minus[:], in0=mean[:], scalar1=minus_mean[:], scalar2=EPS, op0=ALU.mult, op1=ALU.add
+        )
         rstd = keep.tile([P, 1], F32)
-        nc.vector.reciprocal(out=rstd[:], in_=std[:])
+        nc.scalar.activation(out=rstd[:], in_=mean_square[:], func=ACT.Abs_reciprocal_sqrt, bias=eps_minus[:])
         shift = keep.tile([P, 1], F32)
         nc.scalar.activation(out=shift[:], in_=minus_mean[:], func=ACT.Identity, scale=rstd[:])
 

@@ -130,9 +130,9 @@ def tile_decoderblock_pb_t_kernel(tc, h2, w_ff1, b_ff1, w_ff2, b_ff2, out):
         load_unit("h", 2)
         load_unit("h", 3)
         load_chunk("h", 2)
-        load_chunk("h", 3)
         load_chunk("w2", 0)
         load_chunk("w2", 1)
+        load_chunk("h", 3)
         for n in range(4, N_BLOCKS):
             load_chunk("h", n)
 
@@ -144,6 +144,8 @@ def tile_decoderblock_pb_t_kernel(tc, h2, w_ff1, b_ff1, w_ff2, b_ff2, out):
         t_banks = {}
         back_banks = {}
         ring_count = [0]
+        drained = [0]
+        DIRECT = (1, 4, 7, 10, 13)
 
         def ring_bank(shape, name):
             ring_count[0] += 1
@@ -217,8 +219,64 @@ def tile_decoderblock_pb_t_kernel(tc, h2, w_ff1, b_ff1, w_ff2, b_ff2, out):
                     op1=ALU.max,
                 )
 
+        def first_product_b(x, c):
+            n, g = divmod(x, F_PASSES)
+            cols = slice(n * BLOCK + c * P, n * BLOCK + (c + 1) * P)
+            a_banks[x, c] = psum_a.tile([P, PACK, P], F32, tag="a", name="a_bank")
+            for v in range(PACK):
+                rows = slice((g * PACK + v) * P, (g * PACK + v + 1) * P)
+                nc.tensor.matmul_mx(
+                    out=a_banks[x, c][:, v, :],
+                    lhsT=w1_codes[:, rows].bitcast(FP8X4),
+                    lhsT_scale=w1_scales[:, rows],
+                    rhs=h_codes[:, cols].bitcast(FP8X4),
+                    rhs_scale=h_scales[:, cols],
+                    start=True,
+                    stop=True,
+                )
+
+        def bias_b(x, c):
+            if c == 0:
+                a_grouped[x] = work.tile([P, BLOCK, PACK], BF16, align_bytes=64, name="a_direct", bufs=1)
+            g = x % F_PASSES
+            bias = b1_col[:, g * PACK : (g + 1) * PACK].unsqueeze(1).to_broadcast([P, P, PACK])
+            nc.vector.tensor_tensor(
+                out=a_grouped[x][:, c * P : (c + 1) * P, :],
+                in0=a_banks[x, c][:].rearrange("p v c -> p c v"),
+                in1=bias,
+                op=ALU.add,
+            )
+
+        def relu_b(x):
+            flat = a_grouped[x][:].rearrange("p c v -> p (c v)")
+            nc.vector.tensor_scalar(out=flat, in0=flat, scalar1=0.0, scalar2=None, op0=ALU.max)
+
+        def drain(on_scalar, refill=True):
+            i = drained[0]
+            drained[0] += 1
+            x, v = divmod(i, PACK)
+            if x >= ROUNDS:
+                return
+            if x in DIRECT:
+                bias_b(x, v)
+            else:
+                relu_out(x, v, on_scalar)
+            if refill:
+                fill(i + 4)
+
+        def fill(i):
+            x, v = divmod(i, PACK)
+            if x >= ROUNDS:
+                return
+            if x in DIRECT:
+                first_product_b(x, v)
+            else:
+                first_product(x, v)
+
         def group_a(x, on_vector):
-            a_grouped[x] = work.tile([P, BLOCK, PACK], BF16, align_bytes=64, name="a_grouped", bufs=1)
+            a_grouped[x] = work.tile(
+                [P, BLOCK, PACK], BF16, align_bytes=64, name="a_grouped", tag="g1" if x > 0 and x % 3 == 0 else "g0", bufs=1
+            )
             if on_vector:
                 nc.vector.tensor_copy(
                     out=a_grouped[x][:].rearrange("p (c i) v -> p c v i", i=4),
@@ -309,77 +367,130 @@ def tile_decoderblock_pb_t_kernel(tc, h2, w_ff1, b_ff1, w_ff2, b_ff2, out):
         first_product(0, 3)
         lay("w1", 2, True)
         lay("w1", 3, False)
-        turn("h", 2)
-        turn("h", 3)
         quantise("w1", 2)
         quantise("w1", 3)
-        lay("h", 2, False)
-        lay("h", 3, False)
+        drain(False)
+        drain(True)
+        drain(False)
+        drain(True)
+        turn("h", 2)
+        turn("h", 3)
         turn("h", 4)
+        lay("h", 2, True)
+        lay("h", 3, True)
+        group_a(0, False)
+        turn("w2", 0)
+        for c in range(4):
+            drain(False, False)
+        lay("h", 4, True)
+        lay("w2", 0, True)
+        turn("w2", 1)
+        turn("h", 5)
+        turn("w2", 2)
+        turn("w2", 3)
+        lay("w2", 1, True)
+        lay("h", 5, False)
         quantise("h", 2)
         quantise("h", 3)
+        lay("w2", 2, True)
+        lay("w2", 3, True)
+        turn("h", 6)
+        turn("h", 7)
+        for c in range(4):
+            fill(8 + c)
+        lay("h", 6, True)
+        lay("h", 7, True)
+        z_next = [0]
+        sp_next = [0]
 
-        for x in range(POOL_FROM):
-            if 0 <= x - 1:
-                quantise_a(x - 1)
-            if HEAD_SLABS <= x + 3 < N_SLABS:
-                quantise("h", x + 3)
+        def feed(limit):
+            if sp_next[0] < min(limit, T_TILES):
+                second_product(sp_next[0], True)
+                sp_next[0] += 1
+
+        def one_add():
+            if z_next[0] < T_TILES:
+                add_residual(z_next[0])
+                z_next[0] += 1
+
+        sq_next = [0]
+
+        def one_square():
+            if sq_next[0] < z_next[0]:
+                square(sq_next[0])
+                sq_next[0] += 1
+
+        QH = {2: (8, 9, 10, 11), 3: (12, 13), 4: (14, 15)}
+        AV = {1: 4, 2: 8, 3: 16, 4: 20, 5: 28}
+        NA = {1: 2, 2: 5, 3: 6, 4: 5, 5: 8}
+        for p in range(1, 6):
+            g0, g1, b = 3 * p - 1, 3 * p, 3 * p + 1
+            units = list(QH.get(p + 1, ()))
+            if p == 1:
+                relu_b(1)
+                quantise("w2", 0)
+                quantise("h", 4)
+                quantise_a(1)
+                quantise("h", 5)
+                quantise("w2", 1)
+                for v in range(PACK):
+                    drain(True)
+                for v in range(PACK):
+                    drain(True)
+                quantise("h", 6)
+                quantise("h", 7)
+                quantise("w2", 2)
+                quantise("w2", 3)
+                quantise_a(0)
+            else:
+                for i in QH.get(p, ()):
+                    quantise("h", i)
+                relu_b(b - 3)
+                quantise_a(g1 - 3)
+                quantise_a(b - 3)
+                quantise_a(g0 - 3)
+            group_a(g0, False)
+            group_a(g1, False)
+            for i in units:
+                if p == 1:
+                    turn("h", i)
+                lay("h", i, True)
+                if sq_next[0] < z_next[0]:
+                    one_square()
+            while sq_next[0] < z_next[0]:
+                one_square()
+            na = NA[p]
+            for c in range(PACK):
+                drain(False)
+                if c > 0:
+                    feed(AV[p])
             for v in range(PACK):
-                relu_out(x, v, True)
-                first_product(x + 1, v)
-            turn("h", x + 5)
-            lay("h", x + 4, True)
-            if 0 <= x - W2_FROM < W_UNITS:
-                turn("w2", x - W2_FROM)
-            group_a(x, True)
-            if 0 <= x - W2_FROM < W_UNITS:
-                lay("w2", x - W2_FROM, False)
-            if 0 <= x - W2_FROM - 1 < W_UNITS:
-                quantise("w2", x - W2_FROM - 1)
-
-        for z in range(D_TILES):
-            second_product(z, True)
-        for v in range(PACK):
-            relu_out(POOL_FROM, v, True)
-            first_product(POOL_FROM + 1, v)
-        for x in range(POOL_FROM, ROUNDS):
-            z0 = (x - POOL_FROM) * D_TILES
-            if x + 3 < N_SLABS:
-                quantise("h", x + 3)
-            quantise_a(x - 1)
-            group_a(x, False)
-            if x + 5 < N_SLABS:
-                turn("h", x + 5)
-            for v in range(PACK - 1):
-                if x + 1 < ROUNDS:
-                    relu_out(x + 1, v, True)
-                if x + 2 < ROUNDS:
-                    first_product(x + 2, v)
-            if x + 4 < N_SLABS:
-                lay("h", x + 4, False)
-            for z in range(max(z0 - D_TILES, 0), z0):
-                square(z)
-            for z in range(z0, z0 + D_TILES):
-                add_residual(z)
-                if z + D_TILES < (ROUNDS - POOL_FROM) * D_TILES:
-                    second_product(z + D_TILES, True)
-            if x + 1 < ROUNDS:
-                relu_out(x + 1, PACK - 1, False)
-            if x + 2 < ROUNDS:
-                first_product(x + 2, PACK - 1)
-
-        n_early = (ROUNDS - POOL_FROM) * D_TILES
-        for z in range(n_early - D_TILES, n_early):
-            square(z)
-        for z in range(n_early, n_early + AHEAD):
-            second_product(z, False)
-        for z in range(n_early, T_TILES):
-            add_residual(z)
-            if z == n_early:
-                quantise_a(ROUNDS - 1)
-            if z + AHEAD < T_TILES:
-                second_product(z + AHEAD, False)
-            square(z)
+                drain(True)
+                if na > 0:
+                    na -= 1
+                    one_add()
+                    feed(AV[p] if na > 2 or True else 0)
+            for i in QH.get(p + 2, ()):
+                turn("h", i)
+            for v in range(PACK):
+                drain(True)
+                if na > 0:
+                    na -= 1
+                    one_add()
+                    feed(AV[p])
+        quantise_a(14)
+        quantise_a(15)
+        while sp_next[0] < min(z_next[0] + AHEAD, T_TILES):
+            second_product(sp_next[0], False)
+            sp_next[0] += 1
+        while z_next[0] < T_TILES:
+            one_add()
+            if sp_next[0] < T_TILES:
+                second_product(sp_next[0], False)
+                sp_next[0] += 1
+            one_square()
+        while sq_next[0] < T_TILES:
+            one_square()
 
         for q in range(PREFILL):
             transpose_back(q)
@@ -406,18 +517,33 @@ def tile_decoderblock_pb_t_kernel(tc, h2, w_ff1, b_ff1, w_ff2, b_ff2, out):
         shift = keep.tile([P, 1], F32)
         nc.scalar.activation(out=shift[:], in_=minus_mean[:], func=ACT.Identity, scale=rstd[:])
 
-        for q in range(N_PIECES):
-            n, s = divmod(q, SUB)
-            if s % 2 == 0:
-                o_rows = chunks.tile([P, 2, D], F32, tag="chunk", name="o_rows")
-            src = back_banks[q][:].rearrange("r (u e) m -> r u m e", e=2)
-            dst = o_rows[:, s % 2, :].rearrange("r (u m e) -> r u m e", u=2, e=2)
+        def scale(q, o_rows, s, halves):
+            src = back_banks[q][:].rearrange("r (u e) m -> r u m e", e=2)[:, halves]
+            dst = o_rows[:, s % 2, :].rearrange("r (u m e) -> r u m e", u=2, e=2)[:, halves]
             if s % 2 == 0:
                 nc.scalar.activation(out=dst, in_=src, func=ACT.Identity, scale=rstd[:], bias=shift[:])
             else:
                 nc.vector.tensor_scalar(
                     out=dst, in0=src, scalar1=minus_mean[:], scalar2=rstd[:], op0=ALU.add, op1=ALU.mult
                 )
+
+        for q in range(N_PIECES):
+            n, s = divmod(q, SUB)
+            if s % 2 == 0:
+                o_rows = chunks.tile([P, 2, D], F32, tag="chunk", name="o_rows")
+            if q < 2:
+                for u in range(2):
+                    scale(q, o_rows, s, slice(u, u + 1))
+            else:
+                scale(q, o_rows, s, slice(0, 2))
+            if q == 1:
+                for u in range(2):
+                    for r in (1, 0):
+                        nc.sync.dma_start(
+                            out=out_blocks[n][:, r * D + u * (D // 2) : r * D + (u + 1) * (D // 2)],
+                            in_=o_rows[:, r, u * (D // 2) : (u + 1) * (D // 2)],
+                        )
+            elif s % 2 == 1:
                 nc.sync.dma_start(
                     out=out_blocks[n][:, (s - 1) * D : (s + 1) * D],
                     in_=o_rows[:].rearrange("r s d -> r (s d)"),

@@ -284,8 +284,8 @@ def tile_decoderblock_pb_t_kernel(tc, h2, w_ff1, b_ff1, w_ff2, b_ff2, out):
                 )
             else:
                 nc.gpsimd.tensor_scalar(
-                    out=a_grouped[x][:],
-                    in0=a_rows[x][:].rearrange("p v c -> p c v"),
+                    out=a_grouped[x][:].rearrange("p (c i) v -> p c v i", i=4),
+                    in0=a_rows[x][:].rearrange("p v (c i) -> p c v i", i=4),
                     scalar1=1.0,
                     scalar2=0.0,
                     op0=ALU.mult,

@@ -47,8 +47,7 @@ def tile_decoderblock_pb_t_kernel(tc, h2, w_ff1, b_ff1, w_ff2, b_ff2, out):
     out_blocks = out.flatten_outer_dims().rearrange("(n r s) d -> n r (s d)", r=P, s=SUB)
 
     with ExitStack() as whole:
-        pinned = {mybir.EngineType.DVE, mybir.EngineType.Activation, mybir.EngineType.Pool, mybir.EngineType.SP}
-        whole.enter_context(tc.manual_schedule(engines=pinned))
+        whole.enter_context(tc.manual_schedule())
         keep = whole.enter_context(tc.tile_pool(name="keep", bufs=1))
         chunks = whole.enter_context(tc.tile_pool(name="chunks", bufs=8))
         work = whole.enter_context(tc.tile_pool(name="work", bufs=2))
@@ -369,12 +368,12 @@ def tile_decoderblock_pb_t_kernel(tc, h2, w_ff1, b_ff1, w_ff2, b_ff2, out):
         lay("w1", 3, False)
         quantise("w1", 2)
         quantise("w1", 3)
-        drain(False)
-        drain(True)
-        drain(False)
-        drain(True)
         turn("h", 2)
         turn("h", 3)
+        drain(False)
+        drain(True)
+        drain(False)
+        drain(True)
         turn("h", 4)
         lay("h", 2, True)
         lay("h", 3, True)
@@ -400,6 +399,8 @@ def tile_decoderblock_pb_t_kernel(tc, h2, w_ff1, b_ff1, w_ff2, b_ff2, out):
             fill(8 + c)
         lay("h", 6, True)
         lay("h", 7, True)
+        turn("h", 8)
+        turn("h", 9)
         z_next = [0]
         sp_next = [0]
 
@@ -435,6 +436,7 @@ def tile_decoderblock_pb_t_kernel(tc, h2, w_ff1, b_ff1, w_ff2, b_ff2, out):
                 quantise("w2", 1)
                 for v in range(PACK):
                     drain(True)
+                turn("h", 10)
                 for v in range(PACK):
                     drain(True)
                 quantise("h", 6)
@@ -452,14 +454,15 @@ def tile_decoderblock_pb_t_kernel(tc, h2, w_ff1, b_ff1, w_ff2, b_ff2, out):
             group_a(g0, False)
             group_a(g1, False)
             for i in units:
-                if p == 1:
+                if p == 1 and i > 10:
                     turn("h", i)
-                lay("h", i, True)
+                lay("h", i, p > 1 or i > 9)
                 if sq_next[0] < z_next[0]:
                     one_square()
             while sq_next[0] < z_next[0]:
                 one_square()
             na = NA[p]
+            feed(AV[p])
             for c in range(PACK):
                 drain(False)
                 if c > 0:

@@ -87,7 +87,7 @@ def tile_decoderblock_pb_t_kernel(tc, h2, w_ff1, b_ff1, w_ff2, b_ff2, out):
         b1_col = keep.tile([P, F_TILES], F32)
         b2_col = keep.tile([P, D_TILES], F32)
         sums = keep.tile([P, T_TILES, 2], F32)
-        t_cols = keep.tile([P, D_TILES, TOKENS], F32)
+        t_cols = keep.tile([P, N_BLOCKS, D_TILES, BLOCK], F32)
 
         h_grouped_words = h_grouped[:].bitcast(F32)
 
@@ -320,7 +320,7 @@ def tile_decoderblock_pb_t_kernel(tc, h2, w_ff1, b_ff1, w_ff2, b_ff2, out):
             n, j = divmod(z, D_TILES)
             cols = slice(n * BLOCK, (n + 1) * BLOCK)
             nc.vector.scalar_tensor_tensor(
-                out=t_cols[:, j, cols],
+                out=t_cols[:, n, j, :],
                 in0=t_banks[z][:],
                 scalar=b2_col[:, j : j + 1],
                 in1=h_grouped[:, cols, j],
@@ -334,15 +334,16 @@ def tile_decoderblock_pb_t_kernel(tc, h2, w_ff1, b_ff1, w_ff2, b_ff2, out):
             squares = work.tile([P, BLOCK], BF16, name="squares")
             nc.scalar.activation(
                 out=squares[:],
-                in_=t_cols[:, j, n * BLOCK : (n + 1) * BLOCK],
+                in_=t_cols[:, n, j, :],
                 func=ACT.Square,
                 accum_out=sums[:, z, 1:2],
             )
 
         def transpose_back(q):
             back_banks[q] = ring_bank([P, D_TILES, P], "back_bank")
+            n, s = divmod(q, SUB)
             for j in range(D_TILES):
-                nc.tensor.transpose(back_banks[q][:, j, :], t_cols[:, j, q * P : (q + 1) * P], ident[:])
+                nc.tensor.transpose(back_banks[q][:, j, :], t_cols[:, n, j, s * P : (s + 1) * P], ident[:])
 
         nc.vector.tensor_copy(out=b1_col[:], in_=b1_bf[:])
         nc.vector.tensor_copy(out=b2_col[:], in_=b2_bf[:])
@@ -520,9 +521,10 @@ def tile_decoderblock_pb_t_kernel(tc, h2, w_ff1, b_ff1, w_ff2, b_ff2, out):
         shift = keep.tile([P, 1], F32)
         nc.scalar.activation(out=shift[:], in_=minus_mean[:], func=ACT.Identity, scale=rstd[:])
 
-        def scale(q, o_rows, s, halves):
+        def scale(q, halves):
+            n, s = divmod(q, SUB)
             src = back_banks[q][:].rearrange("r (u e) m -> r u m e", e=2)[:, halves]
-            dst = o_rows[:, s % 2, :].rearrange("r (u m e) -> r u m e", u=2, e=2)[:, halves]
+            dst = t_cols[:, n, s, :].rearrange("r (u m e) -> r u m e", u=2, e=2)[:, halves]
             if s % 2 == 0:
                 nc.scalar.activation(out=dst, in_=src, func=ACT.Identity, scale=rstd[:], bias=shift[:])
             else:
@@ -530,26 +532,24 @@ def tile_decoderblock_pb_t_kernel(tc, h2, w_ff1, b_ff1, w_ff2, b_ff2, out):
                     out=dst, in0=src, scalar1=minus_mean[:], scalar2=rstd[:], op0=ALU.add, op1=ALU.mult
                 )
 
+        def store(n, first, last):
+            rows = t_cols[:, n, :, :].rearrange("r s d -> r (s d)")
+            nc.sync.dma_start(out=out_blocks[n][:, first:last], in_=rows[:, first:last])
+
         for q in range(N_PIECES):
             n, s = divmod(q, SUB)
-            if s % 2 == 0:
-                o_rows = chunks.tile([P, 2, D], F32, tag="chunk", name="o_rows")
             if q < 2:
                 for u in range(2):
-                    scale(q, o_rows, s, slice(u, u + 1))
+                    scale(q, slice(u, u + 1))
             else:
-                scale(q, o_rows, s, slice(0, 2))
+                scale(q, slice(0, 2))
             if q == 1:
                 for u in range(2):
                     for r in (1, 0):
-                        nc.sync.dma_start(
-                            out=out_blocks[n][:, r * D + u * (D // 2) : r * D + (u + 1) * (D // 2)],
-                            in_=o_rows[:, r, u * (D // 2) : (u + 1) * (D // 2)],
-                        )
-            elif s % 2 == 1:
-                nc.sync.dma_start(
-                    out=out_blocks[n][:, (s - 1) * D : (s + 1) * D],
-                    in_=o_rows[:].rearrange("r s d -> r (s d)"),
-                )
+                        store(0, r * D + u * (D // 2), r * D + (u + 1) * (D // 2))
+            elif s % 2 == 1 and n in (0, 1, N_BLOCKS - 1):
+                store(n, (s - 1) * D, (s + 1) * D)
+            elif s == SUB - 1:
+                store(n, 0, SUB * D)
             if q + PREFILL < N_PIECES:
                 transpose_back(q + PREFILL)

@@ -55,16 +55,10 @@ def tile_decoderblock_pb_t_kernel(tc, h2, w_ff1, b_ff1, w_ff2, b_ff2, out):
         psum_x = whole.enter_context(tc.psum_pool(name="psum_x", bufs=4))
         psum_a = whole.enter_context(tc.psum_pool(name="psum_a", bufs=4))
 
-        b1_bf = keep.tile([P, F_TILES], BF16)
-        nc.scalar.dma_start(
-            out=b1_bf[:].rearrange("m (c e) -> m c e", e=2),
-            in_=b_ff1.rearrange("(c m e) -> m c e", m=P, e=2),
-        )
-        b2_bf = keep.tile([P, D_TILES], BF16)
-        nc.scalar.dma_start(
-            out=b2_bf[:].rearrange("m (u e) -> m u e", e=2),
-            in_=b_ff2.rearrange("(u m e) -> m u e", m=P, e=2),
-        )
+        bias_rows = keep.tile([P, 2 * P], BF16)
+        nc.vector.memset(bias_rows[:], 0.0)
+        nc.scalar.dma_start(out=bias_rows[0:4, :], in_=b_ff1.rearrange("(c x) -> c x", c=4))
+        nc.scalar.dma_start(out=bias_rows[4:6, :], in_=b_ff2.rearrange("(c x) -> c x", c=2))
 
         ident = keep.tile([P, P], F32)
         make_identity(nc, ident[:])
@@ -84,9 +78,11 @@ def tile_decoderblock_pb_t_kernel(tc, h2, w_ff1, b_ff1, w_ff2, b_ff2, out):
         w1_scales = keep.tile([P, F_TILES * P], U8, align_bytes=64)
         w2_codes = keep.tile([P, D_TILES * F_PASSES * P], U32, align_bytes=64)
         w2_scales = keep.tile([P, D_TILES * F_PASSES * P], U8, align_bytes=64)
-        b1_col = keep.tile([P, F_TILES], F32)
-        b2_col = keep.tile([P, D_TILES], F32)
+        bias_cols = keep.tile([P, F_TILES + D_TILES], F32)
+        b1_col = bias_cols[:, 0:F_TILES]
+        b2_col = bias_cols[:, F_TILES : F_TILES + D_TILES]
         sums = keep.tile([P, T_TILES, 2], F32)
+        last_squares = keep.tile([P, 2], F32)
         t_cols = keep.tile([P, N_BLOCKS, D_TILES, BLOCK], F32)
 
         h_grouped_words = h_grouped[:].bitcast(F32)
@@ -183,6 +179,14 @@ def tile_decoderblock_pb_t_kernel(tc, h2, w_ff1, b_ff1, w_ff2, b_ff2, out):
                 out=codes[:, cols].bitcast(FP8X4),
                 scales=scales[:, cols],
                 in_=grouped.rearrange("p c v -> p (c v)"),
+            )
+
+        def quantise_block(n):
+            cols = slice(n * BLOCK, (n + 1) * BLOCK)
+            nc.vector.quantize_mx(
+                out=h_codes[:, cols].bitcast(FP8X4),
+                scales=h_scales[:, cols],
+                in_=h_grouped[:, cols, :].rearrange("p c v -> p (c v)"),
             )
 
         def first_product(x, v):
@@ -339,14 +343,29 @@ def tile_decoderblock_pb_t_kernel(tc, h2, w_ff1, b_ff1, w_ff2, b_ff2, out):
                 accum_out=sums[:, z, 1:2],
             )
 
+        def square_last():
+            half = BLOCK // 2
+            tile = t_cols[:, N_BLOCKS - 1, D_TILES - 1, :]
+            squares = work.tile([P, BLOCK], BF16, name="squares")
+            nc.scalar.activation(
+                out=squares[:, 0:half], in_=tile[:, 0:half], func=ACT.Square, accum_out=last_squares[:, 0:1]
+            )
+            nc.vector.scalar_tensor_tensor(
+                out=squares[:, half:BLOCK],
+                in0=tile[:, half:BLOCK],
+                scalar=1.0,
+                in1=tile[:, half:BLOCK],
+                op0=ALU.mult,
+                op1=ALU.mult,
+                accum_out=last_squares[:, 1:2],
+            )
+
         def transpose_back(q):
             back_banks[q] = ring_bank([P, D_TILES, P], "back_bank")
             n, s = divmod(q, SUB)
             for j in range(D_TILES):
                 nc.tensor.transpose(back_banks[q][:, j, :], t_cols[:, n, j, s * P : (s + 1) * P], ident[:])
 
-        nc.vector.tensor_copy(out=b1_col[:], in_=b1_bf[:])
-        nc.vector.tensor_copy(out=b2_col[:], in_=b2_bf[:])
         turn("w1", 0)
         lay("w1", 0, True)
         turn("h", 0)
@@ -360,6 +379,8 @@ def tile_decoderblock_pb_t_kernel(tc, h2, w_ff1, b_ff1, w_ff2, b_ff2, out):
         quantise("h", 1)
         turn("w1", 2)
         turn("w1", 3)
+        bias_bank = psum_x.tile([P, P], F32, tag="x", name="bias_bank")
+        nc.tensor.transpose(bias_bank[:], bias_rows[:].bitcast(F32), ident[:])
         first_product(0, 0)
         first_product(0, 1)
         quantise("w1", 1)
@@ -368,12 +389,13 @@ def tile_decoderblock_pb_t_kernel(tc, h2, w_ff1, b_ff1, w_ff2, b_ff2, out):
         lay("w1", 2, True)
         lay("w1", 3, False)
         quantise("w1", 2)
+        nc.vector.tensor_copy(out=bias_cols[:], in_=bias_bank[:].bitcast(BF16)[:, 0 : F_TILES + D_TILES])
         quantise("w1", 3)
         turn("h", 2)
         turn("h", 3)
-        drain(False)
         drain(True)
         drain(False)
+        drain(True)
         drain(True)
         turn("h", 4)
         lay("h", 2, True)
@@ -390,8 +412,7 @@ def tile_decoderblock_pb_t_kernel(tc, h2, w_ff1, b_ff1, w_ff2, b_ff2, out):
         turn("w2", 3)
         lay("w2", 1, True)
         lay("h", 5, False)
-        quantise("h", 2)
-        quantise("h", 3)
+        quantise_block(1)
         lay("w2", 2, True)
         lay("w2", 3, True)
         turn("h", 6)
@@ -440,14 +461,13 @@ def tile_decoderblock_pb_t_kernel(tc, h2, w_ff1, b_ff1, w_ff2, b_ff2, out):
                 turn("h", 10)
                 for v in range(PACK):
                     drain(True)
-                quantise("h", 6)
-                quantise("h", 7)
+                quantise_block(3)
                 quantise("w2", 2)
                 quantise("w2", 3)
                 quantise_a(0)
             else:
-                for i in QH.get(p, ()):
-                    quantise("h", i)
+                for i in QH.get(p, ())[::2]:
+                    quantise_block(i // 2)
                 relu_b(b - 3)
                 quantise_a(g1 - 3)
                 quantise_a(b - 3)
@@ -492,11 +512,12 @@ def tile_decoderblock_pb_t_kernel(tc, h2, w_ff1, b_ff1, w_ff2, b_ff2, out):
             if sp_next[0] < T_TILES:
                 second_product(sp_next[0], False)
                 sp_next[0] += 1
-            one_square()
-        while sq_next[0] < T_TILES:
+            if sq_next[0] < T_TILES - 1:
+                one_square()
+        while sq_next[0] < T_TILES - 1:
             one_square()
 
-        for q in range(PREFILL):
+        for q in range(SUB):
             transpose_back(q)
 
         stat = keep.tile([P, 2], F32)
@@ -504,18 +525,20 @@ def tile_decoderblock_pb_t_kernel(tc, h2, w_ff1, b_ff1, w_ff2, b_ff2, out):
         mean = ring_bank([P, 1], "mean")
         nc.tensor.matmul(out=mean[:], lhsT=averager[:], rhs=stat[:, 0:1], start=True, stop=False)
         nc.tensor.matmul(out=mean[:], lhsT=averager[:], rhs=sums[:, T_TILES - 1, 0:1], start=False, stop=True)
+        square_last()
         nc.vector.tensor_reduce(out=stat[:, 1:2], in_=sums[:, 0 : T_TILES - 1, 1], axis=AXIS_X, op=ALU.add)
         mean_square = ring_bank([P, 1], "mean_square")
         nc.tensor.matmul(out=mean_square[:], lhsT=averager[:], rhs=stat[:, 1:2], start=True, stop=False)
-        nc.tensor.matmul(
-            out=mean_square[:], lhsT=averager[:], rhs=sums[:, T_TILES - 1, 1:2], start=False, stop=True
-        )
+        nc.tensor.matmul(out=mean_square[:], lhsT=averager[:], rhs=last_squares[:, 1:2], start=False, stop=False)
+        nc.tensor.matmul(out=mean_square[:], lhsT=averager[:], rhs=last_squares[:, 0:1], start=False, stop=True)
         minus_mean = keep.tile([P, 1], F32)
         nc.vector.tensor_scalar(out=minus_mean[:], in0=mean[:], scalar1=-1.0, scalar2=None, op0=ALU.mult)
         eps_minus = keep.tile([P, 1], F32)
         nc.vector.tensor_scalar(
             out=eps_minus[:], in0=mean[:], scalar1=minus_mean[:], scalar2=EPS, op0=ALU.mult, op1=ALU.add
         )
+        for q in range(SUB, PREFILL):
+            transpose_back(q)
         rstd = keep.tile([P, 1], F32)
         nc.scalar.activation(out=rstd[:], in_=mean_square[:], func=ACT.Abs_reciprocal_sqrt, bias=eps_minus[:])
         shift = keep.tile([P, 1], F32)

@@ -57,6 +57,8 @@ def tile_decoderblock_pb_t_kernel(tc, h2, w_ff1, b_ff1, w_ff2, b_ff2, out):
 
         bias_rows = keep.tile([P, 2 * P], BF16)
         nc.vector.memset(bias_rows[:], 0.0)
+        zeros = keep.tile([P, BLOCK], BF16)
+        nc.vector.memset(zeros[:], 0.0)
         nc.scalar.dma_start(out=bias_rows[0:4, :], in_=b_ff1.rearrange("(c x) -> c x", c=4))
         nc.scalar.dma_start(out=bias_rows[4:6, :], in_=b_ff2.rearrange("(c x) -> c x", c=2))
 
@@ -366,14 +368,23 @@ def tile_decoderblock_pb_t_kernel(tc, h2, w_ff1, b_ff1, w_ff2, b_ff2, out):
             for j in range(D_TILES):
                 nc.tensor.transpose(back_banks[q][:, j, :], t_cols[:, n, j, s * P : (s + 1) * P], ident[:])
 
+        def keep_busy(n):
+            bank = psum_a.tile([P, BLOCK], F32, tag="a", name="idle_bank")
+            for i in range(n):
+                nc.tensor.matmul(out=bank[:], lhsT=zeros[:, 0:P], rhs=zeros[:], start=True, stop=True)
+
+        keep_busy(4)
         turn("w1", 0)
+        keep_busy(1)
         lay("w1", 0, True)
         turn("h", 0)
         lay("h", 0, False)
         turn("h", 1)
+        keep_busy(1)
         quantise("w1", 0)
         lay("h", 1, True)
         turn("w1", 1)
+        keep_busy(1)
         quantise("h", 0)
         lay("w1", 1, True)
         quantise("h", 1)

@@ -52,8 +52,7 @@ def tile_decoderblock_pb_t_kernel(tc, h2, w_ff1, b_ff1, w_ff2, b_ff2, out):
         chunks = whole.enter_context(tc.tile_pool(name="chunks", bufs=8))
         work = whole.enter_context(tc.tile_pool(name="work", bufs=2))
         w_work = whole.enter_context(tc.tile_pool(name="w_work", bufs=4))
-        psum_x = whole.enter_context(tc.psum_pool(name="psum_x", bufs=4))
-        psum_a = whole.enter_context(tc.psum_pool(name="psum_a", bufs=4))
+        psum_x = whole.enter_context(tc.psum_pool(name="psum_x", bufs=8))
 
         bias_rows = keep.tile([P, 2 * P], BF16)
         nc.vector.memset(bias_rows[:], 0.0)
@@ -140,15 +139,11 @@ def tile_decoderblock_pb_t_kernel(tc, h2, w_ff1, b_ff1, w_ff2, b_ff2, out):
         a_grouped = {}
         t_banks = {}
         back_banks = {}
-        ring_count = [0]
         drained = [0]
         DIRECT = (1, 4, 7, 10, 13)
 
         def ring_bank(shape, name):
-            ring_count[0] += 1
-            if ring_count[0] % 2 == 1:
-                return psum_x.tile(shape, F32, tag="x", name=name)
-            return psum_a.tile(shape, F32, tag="a", name=name)
+            return psum_x.tile(shape, F32, tag="x", name=name)
 
         def turn(kind, i):
             words = raw_words[kind, i // 2][:, (i % 2) * 4 * P : (i % 2 + 1) * 4 * P]
@@ -195,7 +190,7 @@ def tile_decoderblock_pb_t_kernel(tc, h2, w_ff1, b_ff1, w_ff2, b_ff2, out):
             n, g = divmod(x, F_PASSES)
             cols = slice(n * BLOCK, (n + 1) * BLOCK)
             rows = slice((g * PACK + v) * P, (g * PACK + v + 1) * P)
-            a_banks[x, v] = psum_a.tile([P, BLOCK], F32, tag="a", name="a_bank")
+            a_banks[x, v] = psum_x.tile([P, BLOCK], F32, tag="x", name="a_bank")
             nc.tensor.matmul_mx(
                 out=a_banks[x, v][:],
                 lhsT=w1_codes[:, rows].bitcast(FP8X4),
@@ -227,7 +222,7 @@ def tile_decoderblock_pb_t_kernel(tc, h2, w_ff1, b_ff1, w_ff2, b_ff2, out):
         def first_product_b(x, c):
             n, g = divmod(x, F_PASSES)
             cols = slice(n * BLOCK + c * P, n * BLOCK + (c + 1) * P)
-            a_banks[x, c] = psum_a.tile([P, PACK, P], F32, tag="a", name="a_bank")
+            a_banks[x, c] = psum_x.tile([P, PACK, P], F32, tag="x", name="a_bank")
             for v in range(PACK):
                 rows = slice((g * PACK + v) * P, (g * PACK + v + 1) * P)
                 nc.tensor.matmul_mx(
@@ -369,7 +364,7 @@ def tile_decoderblock_pb_t_kernel(tc, h2, w_ff1, b_ff1, w_ff2, b_ff2, out):
                 nc.tensor.transpose(back_banks[q][:, j, :], t_cols[:, n, j, s * P : (s + 1) * P], ident[:])
 
         def keep_busy(n):
-            bank = psum_a.tile([P, BLOCK], F32, tag="a", name="idle_bank")
+            bank = psum_x.tile([P, BLOCK], F32, tag="x", name="idle_bank")
             for i in range(n):
                 nc.tensor.matmul(out=bank[:], lhsT=zeros[:, 0:P], rhs=zeros[:], start=True, stop=True)
 
@@ -384,14 +379,15 @@ def tile_decoderblock_pb_t_kernel(tc, h2, w_ff1, b_ff1, w_ff2, b_ff2, out):
         quantise("w1", 0)
         lay("h", 1, True)
         turn("w1", 1)
+        bias_bank = psum_x.tile([P, P], F32, tag="x", name="bias_bank")
+        nc.tensor.transpose(bias_bank[:], bias_rows[:].bitcast(F32), ident[:])
         keep_busy(1)
         quantise("h", 0)
         lay("w1", 1, True)
+        nc.vector.tensor_copy(out=bias_cols[:], in_=bias_bank[:].bitcast(BF16)[:, 0 : F_TILES + D_TILES])
         quantise("h", 1)
         turn("w1", 2)
         turn("w1", 3)
-        bias_bank = psum_x.tile([P, P], F32, tag="x", name="bias_bank")
-        nc.tensor.transpose(bias_bank[:], bias_rows[:].bitcast(F32), ident[:])
         first_product(0, 0)
         first_product(0, 1)
         quantise("w1", 1)
@@ -400,7 +396,6 @@ def tile_decoderblock_pb_t_kernel(tc, h2, w_ff1, b_ff1, w_ff2, b_ff2, out):
         lay("w1", 2, True)
         lay("w1", 3, False)
         quantise("w1", 2)
-        nc.vector.tensor_copy(out=bias_cols[:], in_=bias_bank[:].bitcast(BF16)[:, 0 : F_TILES + D_TILES])
         quantise("w1", 3)
         turn("h", 2)
         turn("h", 3)

from contextlib import ExitStack

import concourse.mybir as mybir
from concourse.masks import make_identity

F32 = mybir.dt.float32
BF16 = mybir.dt.bfloat16
U32 = mybir.dt.uint32
U8 = mybir.dt.uint8
FP8X4 = mybir.dt.float8_e4m3fn_x4
ACT = mybir.ActivationFunctionType
ALU = mybir.AluOpType
AXIS_X = mybir.AxisListType.X

P = 128
PACK = 4
D = 512
F = 1024
TOKENS = 2 * 2048
BLOCK = 512
SUB = BLOCK // P
UNIT = 2 * P
CHUNK = 2048
N_BLOCKS = TOKENS // BLOCK
N_SLABS = TOKENS // UNIT
N_PIECES = TOKENS // P
F_TILES = F // P
D_TILES = D // P
F_PASSES = F // (P * PACK)
W_UNITS = 4
ROUNDS = N_BLOCKS * F_PASSES
T_TILES = N_BLOCKS * D_TILES
HEAD_SLABS = 4
W2_FROM = 2
POOL_FROM = 10
AHEAD = 4
PREFILL = 6
EPS = 1e-5

FLOPS = 2 * TOKENS * D * F * 2


def tile_decoderblock_pb_t_kernel(tc, h2, w_ff1, b_ff1, w_ff2, b_ff2, out):
    nc = tc.nc

    h_blocks = h2.flatten_outer_dims().rearrange("(n r s) d -> n r (s d)", r=P, s=SUB)
    out_blocks = out.flatten_outer_dims().rearrange("(n r s) d -> n r (s d)", r=P, s=SUB)

    with ExitStack() as whole:
        whole.enter_context(tc.manual_schedule())
        keep = whole.enter_context(tc.tile_pool(name="keep", bufs=1))
        chunks = whole.enter_context(tc.tile_pool(name="chunks", bufs=8))
        work = whole.enter_context(tc.tile_pool(name="work", bufs=2))
        w_work = whole.enter_context(tc.tile_pool(name="w_work", bufs=4))
        psum_x = whole.enter_context(tc.psum_pool(name="psum_x", bufs=8))

        bias_rows = keep.tile([P, 2 * P], BF16)
        nc.vector.memset(bias_rows[:], 0.0)
        zeros = keep.tile([P, BLOCK], BF16)
        nc.vector.memset(zeros[:], 0.0)
        nc.scalar.dma_start(out=bias_rows[0:4, :], in_=b_ff1.rearrange("(c x) -> c x", c=4))
        nc.scalar.dma_start(out=bias_rows[4:6, :], in_=b_ff2.rearrange("(c x) -> c x", c=2))

        ident = keep.tile([P, P], F32)
        make_identity(nc, ident[:])
        averager = keep.tile([P, P], F32)
        nc.vector.memset(averager[:], 1.0 / (TOKENS * D))
        warm_in = keep.tile([P, 1], F32)
        nc.vector.memset(warm_in[:], 1.0)
        table_warm = keep.tile([P, 1], F32)
        nc.scalar.activation(out=table_warm[:], in_=warm_in[:], func=ACT.Abs_reciprocal_sqrt)

        h_grouped = keep.tile([P, TOKENS, PACK], BF16, align_bytes=64)
        h_codes = keep.tile([P, TOKENS], U32, align_bytes=64)
        h_scales = keep.tile([P, TOKENS], U8, align_bytes=64)
        a_codes = keep.tile([P, ROUNDS, BLOCK], U32, align_bytes=64)
        a_scales = keep.tile([P, ROUNDS, BLOCK], U8, align_bytes=64)
        w1_codes = keep.tile([P, F_TILES * P], U32, align_bytes=64)
        w1_scales = keep.tile([P, F_TILES * P], U8, align_bytes=64)
        w2_codes = keep.tile([P, D_TILES * F_PASSES * P], U32, align_bytes=64)
        w2_scales = keep.tile([P, D_TILES * F_PASSES * P], U8, align_bytes=64)
        bias_cols = keep.tile([P, F_TILES + D_TILES], F32)
        b1_col = bias_cols[:, 0:F_TILES]
        b2_col = bias_cols[:, F_TILES : F_TILES + D_TILES]
        sums = keep.tile([P, T_TILES, 2], F32)
        last_squares = keep.tile([P, 2], F32)
        t_cols = keep.tile([P, N_BLOCKS, D_TILES, BLOCK], F32)

        h_grouped_words = h_grouped[:].bitcast(F32)

        raw_tiles = {}
        raw_words = {}

        def rows_of(kind, c):
            if kind == "h":
                return h_blocks[c]
            if kind == "w1":
                return w_ff1[c * 2 * UNIT : (c + 1) * 2 * UNIT, :].rearrange("(u m e) d -> m u (e d)", m=P, e=2)
            return w_ff2[c * UNIT : (c + 1) * UNIT, :].rearrange("(m e) f -> m (e f)", e=2)

        def chunk_tile(kind, c):
            if (kind, c) not in raw_tiles:
                raw_tiles[kind, c] = chunks.tile([P, CHUNK], BF16, tag="chunk", name="raw")
                raw_words[kind, c] = raw_tiles[kind, c][:].bitcast(F32)
            return raw_tiles[kind, c]

        def load_chunk(kind, c):
            dst = chunk_tile(kind, c)[:]
            if kind == "w1":
                dst = dst.rearrange("m (u x) -> m u x", u=2)
            nc.sync.dma_start(out=dst, in_=rows_of(kind, c))

        def load_unit(kind, i):
            half = slice((i % 2) * (CHUNK // 2), (i % 2 + 1) * (CHUNK // 2))
            if kind == "w1":
                rows = rows_of(kind, i // 2)[:, i % 2, :]
            else:
                rows = rows_of(kind, i // 2)[:, half]
            nc.sync.dma_start(out=chunk_tile(kind, i // 2)[:, half], in_=rows)

        load_unit("w1", 0)
        load_unit("h", 0)
        load_unit("h", 1)
        for i in range(1, W_UNITS):
            load_unit("w1", i)
        load_unit("h", 2)
        load_unit("h", 3)
        load_chunk("h", 2)
        load_chunk("w2", 0)
        load_chunk("w2", 1)
        load_chunk("h", 3)
        for n in range(4, N_BLOCKS):
            load_chunk("h", n)

        x_banks = {}
        w_grouped = {}
        a_banks = {}
        a_rows = {}
        a_grouped = {}
        t_banks = {}
        back_banks = {}
        drained = [0]
        DIRECT = (1, 4, 7, 10, 13)

        def ring_bank(shape, name):
            return psum_x.tile(shape, F32, tag="x", name=name)

        def turn(kind, i):
            words = raw_words[kind, i // 2][:, (i % 2) * 4 * P : (i % 2 + 1) * 4 * P]
            x_banks[kind, i] = psum_x.tile([P, 4, P], F32, tag="x", name="x_bank")
            for k in range(4):
                nc.tensor.transpose(x_banks[kind, i][:, k, :], words[:, k * P : (k + 1) * P], ident[:])

        def lay(kind, i, on_scalar):
            if kind == "h":
                grouped_words = h_grouped_words[:, i * UNIT : (i + 1) * UNIT, :]
            else:
                w_grouped[kind, i] = w_work.tile([P, UNIT, PACK], BF16, align_bytes=64, name="w_grouped")
                grouped_words = w_grouped[kind, i][:].bitcast(F32)
            dst = grouped_words.rearrange("p (a r) u -> p a r u", a=2)
            src = x_banks[kind, i][:].rearrange("p (a u) r -> p a r u", u=2)
            if on_scalar:
                nc.scalar.copy(out=dst, in_=src)
            else:
                nc.vector.tensor_copy(out=dst, in_=src)

        def quantise(kind, i):
            cols = slice(i * UNIT, (i + 1) * UNIT)
            if kind == "h":
                codes, scales, grouped = h_codes, h_scales, h_grouped[:, cols, :]
            elif kind == "w1":
                codes, scales, grouped = w1_codes, w1_scales, w_grouped[kind, i][:]
            else:
                codes, scales, grouped = w2_codes, w2_scales, w_grouped[kind, i][:]
            nc.vector.quantize_mx(
                out=codes[:, cols].bitcast(FP8X4),
                scales=scales[:, cols],
                in_=grouped.rearrange("p c v -> p (c v)"),
            )

        def quantise_block(n):
            cols = slice(n * BLOCK, (n + 1) * BLOCK)
            nc.vector.quantize_mx(
                out=h_codes[:, cols].bitcast(FP8X4),
                scales=h_scales[:, cols],
                in_=h_grouped[:, cols, :].rearrange("p c v -> p (c v)"),
            )

        def first_product(x, v):
            n, g = divmod(x, F_PASSES)
            cols = slice(n * BLOCK, (n + 1) * BLOCK)
            rows = slice((g * PACK + v) * P, (g * PACK + v + 1) * P)
            a_banks[x, v] = psum_x.tile([P, BLOCK], F32, tag="x", name="a_bank")
            nc.tensor.matmul_mx(
                out=a_banks[x, v][:],
                lhsT=w1_codes[:, rows].bitcast(FP8X4),
                lhsT_scale=w1_scales[:, rows],
                rhs=h_codes[:, cols].bitcast(FP8X4),
                rhs_scale=h_scales[:, cols],
                start=True,
                stop=True,
            )

        def relu_out(x, v, on_scalar):
            if v == 0:
                a_rows[x] = work.tile([P, PACK, BLOCK], BF16, name="a_rows", bufs=3)
            i = (x % F_PASSES) * PACK + v
            if on_scalar:
                nc.scalar.activation(
                    out=a_rows[x][:, v, :], in_=a_banks[x, v][:], func=ACT.Relu, bias=b1_col[:, i : i + 1]
                )
            else:
                nc.vector.tensor_scalar(
                    out=a_rows[x][:, v, :],
                    in0=a_banks[x, v][:],
                    scalar1=b1_col[:, i : i + 1],
                    scalar2=0.0,
                    op0=ALU.add,
                    op1=ALU.max,
                )

        def first_product_b(x, c):
            n, g = divmod(x, F_PASSES)
            cols = slice(n * BLOCK + c * P, n * BLOCK + (c + 1) * P)
            a_banks[x, c] = psum_x.tile([P, PACK, P], F32, tag="x", name="a_bank")
            for v in range(PACK):
                rows = slice((g * PACK + v) * P, (g * PACK + v + 1) * P)
                nc.tensor.matmul_mx(
                    out=a_banks[x, c][:, v, :],
                    lhsT=w1_codes[:, rows].bitcast(FP8X4),
                    lhsT_scale=w1_scales[:, rows],
                    rhs=h_codes[:, cols].bitcast(FP8X4),
                    rhs_scale=h_scales[:, cols],
                    start=True,
                    stop=True,
                )

        def bias_b(x, c):
            if c == 0:
                a_grouped[x] = work.tile([P, BLOCK, PACK], BF16, align_bytes=64, name="a_direct", bufs=1)
            g = x % F_PASSES
            bias = b1_col[:, g * PACK : (g + 1) * PACK].unsqueeze(1).to_broadcast([P, P, PACK])
            nc.vector.tensor_tensor(
                out=a_grouped[x][:, c * P : (c + 1) * P, :],
                in0=a_banks[x, c][:].rearrange("p v c -> p c v"),
                in1=bias,
                op=ALU.add,
            )

        def relu_b(x):
            flat = a_grouped[x][:].rearrange("p c v -> p (c v)")
            nc.vector.tensor_scalar(out=flat, in0=flat, scalar1=0.0, scalar2=None, op0=ALU.max)

        def drain(on_scalar, refill=True):
            i = drained[0]
            drained[0] += 1
            x, v = divmod(i, PACK)
            if x >= ROUNDS:
                return
            if x in DIRECT:
                bias_b(x, v)
            else:
                relu_out(x, v, on_scalar)
            if refill:
                fill(i + 4)

        def fill(i):
            x, v = divmod(i, PACK)
            if x >= ROUNDS:
                return
            if x in DIRECT:
                first_product_b(x, v)
            else:
                first_product(x, v)

        def group_a(x, on_vector):
            a_grouped[x] = work.tile(
                [P, BLOCK, PACK], BF16, align_bytes=64, name="a_grouped", tag="g1" if x > 0 and x % 3 == 0 else "g0", bufs=1
            )
            if on_vector:
                nc.vector.tensor_copy(
                    out=a_grouped[x][:].rearrange("p (c i) v -> p c v i", i=4),
                    in_=a_rows[x][:].rearrange("p v (c i) -> p c v i", i=4),
                )
            else:
                nc.gpsimd.tensor_scalar(
                    out=a_grouped[x][:].rearrange("p (c i) v -> p c v i", i=4),
                    in0=a_rows[x][:].rearrange("p v (c i) -> p c v i", i=4),
                    scalar1=1.0,
                    scalar2=0.0,
                    op0=ALU.mult,
                    op1=ALU.add,
                )

        def quantise_a(x):
            nc.vector.quantize_mx(
                out=a_codes[:, x, :].bitcast(FP8X4),
                scales=a_scales[:, x, :],
                in_=a_grouped[x][:].rearrange("p c v -> p (c v)"),
            )

        def second_product(z, early):
            n, j = divmod(z, D_TILES)
            if early:
                t_banks[z] = psum_x.tile([P, BLOCK], F32, tag="x", name="t_bank")
            else:
                t_banks[z] = ring_bank([P, BLOCK], "t_bank")
            for g in range(F_PASSES):
                rows = slice((j * F_PASSES + g) * P, (j * F_PASSES + g + 1) * P)
                nc.tensor.matmul_mx(
                    out=t_banks[z][:],
                    lhsT=w2_codes[:, rows].bitcast(FP8X4),
                    lhsT_scale=w2_scales[:, rows],
                    rhs=a_codes[:, n * F_PASSES + g, :].bitcast(FP8X4),
                    rhs_scale=a_scales[:, n * F_PASSES + g, :],
                    start=(g == 0),
                    stop=(g == F_PASSES - 1),
                )

        def add_residual(z):
            n, j = divmod(z, D_TILES)
            cols = slice(n * BLOCK, (n + 1) * BLOCK)
            nc.vector.scalar_tensor_tensor(
                out=t_cols[:, n, j, :],
                in0=t_banks[z][:],
                scalar=b2_col[:, j : j + 1],
                in1=h_grouped[:, cols, j],
                op0=ALU.add,
                op1=ALU.add,
                accum_out=sums[:, z, 0:1],
            )

        def square(z):
            n, j = divmod(z, D_TILES)
            squares = work.tile([P, BLOCK], BF16, name="squares")
            nc.scalar.activation(
                out=squares[:],
                in_=t_cols[:, n, j, :],
                func=ACT.Square,
                accum_out=sums[:, z, 1:2],
            )

        def square_last():
            half = BLOCK // 2
            tile = t_cols[:, N_BLOCKS - 1, D_TILES - 1, :]
            squares = work.tile([P, BLOCK], BF16, name="squares")
            nc.scalar.activation(
                out=squares[:, 0:half], in_=tile[:, 0:half], func=ACT.Square, accum_out=last_squares[:, 0:1]
            )
            nc.vector.scalar_tensor_tensor(
                out=squares[:, half:BLOCK],
                in0=tile[:, half:BLOCK],
                scalar=1.0,
                in1=tile[:, half:BLOCK],
                op0=ALU.mult,
                op1=ALU.mult,
                accum_out=last_squares[:, 1:2],
            )

        def transpose_back(q):
            back_banks[q] = ring_bank([P, D_TILES, P], "back_bank")
            n, s = divmod(q, SUB)
            for j in range(D_TILES):
                nc.tensor.transpose(back_banks[q][:, j, :], t_cols[:, n, j, s * P : (s + 1) * P], ident[:])

        def keep_busy(n):
            bank = psum_x.tile([P, BLOCK], F32, tag="x", name="idle_bank")
            for i in range(n):
                nc.tensor.matmul(out=bank[:], lhsT=zeros[:, 0:P], rhs=zeros[:], start=True, stop=True)

        keep_busy(4)
        turn("w1", 0)
        keep_busy(1)
        lay("w1", 0, True)
        turn("h", 0)
        lay("h", 0, False)
        turn("h", 1)
        keep_busy(1)
        quantise("w1", 0)
        lay("h", 1, True)
        turn("w1", 1)
        bias_bank = psum_x.tile([P, P], F32, tag="x", name="bias_bank")
        nc.tensor.transpose(bias_bank[:], bias_rows[:].bitcast(F32), ident[:])
        keep_busy(1)
        quantise("h", 0)
        lay("w1", 1, True)
        nc.vector.tensor_copy(out=bias_cols[:], in_=bias_bank[:].bitcast(BF16)[:, 0 : F_TILES + D_TILES])
        quantise("h", 1)
        turn("w1", 2)
        turn("w1", 3)
        first_product(0, 0)
        first_product(0, 1)
        quantise("w1", 1)
        first_product(0, 2)
        first_product(0, 3)
        lay("w1", 2, True)
        lay("w1", 3, False)
        quantise("w1", 2)
        quantise("w1", 3)
        turn("h", 2)
        turn("h", 3)
        drain(True)
        drain(False)
        drain(True)
        drain(True)
        turn("h", 4)
        lay("h", 2, True)
        lay("h", 3, True)
        group_a(0, False)
        turn("w2", 0)
        for c in range(4):
            drain(False, False)
        lay("h", 4, True)
        lay("w2", 0, True)
        turn("w2", 1)
        turn("h", 5)
        turn("w2", 2)
        turn("w2", 3)
        lay("w2", 1, True)
        lay("h", 5, False)
        quantise_block(1)
        lay("w2", 2, True)
        lay("w2", 3, True)
        turn("h", 6)
        turn("h", 7)
        for c in range(4):
            fill(8 + c)
        lay("h", 6, True)
        lay("h", 7, True)
        turn("h", 8)
        turn("h", 9)
        z_next = [0]
        sp_next = [0]

        def feed(limit):
            if sp_next[0] < min(limit, T_TILES):
                second_product(sp_next[0], True)
                sp_next[0] += 1

        def one_add():
            if z_next[0] < T_TILES:
                add_residual(z_next[0])
                z_next[0] += 1

        sq_next = [0]

        def one_square():
            if sq_next[0] < z_next[0]:
                square(sq_next[0])
                sq_next[0] += 1

        QH = {2: (8, 9, 10, 11), 3: (12, 13), 4: (14, 15)}
        AV = {1: 4, 2: 8, 3: 16, 4: 20, 5: 28}
        NA = {1: 2, 2: 5, 3: 6, 4: 5, 5: 8}
        for p in range(1, 6):
            g0, g1, b = 3 * p - 1, 3 * p, 3 * p + 1
            units = list(QH.get(p + 1, ()))
            if p == 1:
                relu_b(1)
                quantise("w2", 0)
                quantise("h", 4)
                quantise_a(1)
                quantise("h", 5)
                quantise("w2", 1)
                for v in range(PACK):
                    drain(True)
                turn("h", 10)
                for v in range(PACK):
                    drain(True)
                quantise_block(3)
                quantise("w2", 2)
                quantise("w2", 3)
                quantise_a(0)
            else:
                for i in QH.get(p, ())[::2]:
                    quantise_block(i // 2)
                relu_b(b - 3)
                quantise_a(g1 - 3)
                quantise_a(b - 3)
                quantise_a(g0 - 3)
            group_a(g0, False)
            group_a(g1, False)
            for i in units:
                if p == 1 and i > 10:
                    turn("h", i)
                lay("h", i, p > 1 or i > 9)
                if sq_next[0] < z_next[0]:
                    one_square()
            while sq_next[0] < z_next[0]:
                one_square()
            na = NA[p]
            feed(AV[p])
            for c in range(PACK):
                drain(False)
                if c > 0:
                    feed(AV[p])
            for v in range(PACK):
                drain(True)
                if na > 0:
                    na -= 1
                    one_add()
                    feed(AV[p] if na > 2 or True else 0)
            for i in QH.get(p + 2, ()):
                turn("h", i)
            for v in range(PACK):
                drain(True)
                if na > 0:
                    na -= 1
                    one_add()
                    feed(AV[p])
        quantise_a(14)
        quantise_a(15)
        while sp_next[0] < min(z_next[0] + AHEAD, T_TILES):
            second_product(sp_next[0], False)
            sp_next[0] += 1
        while z_next[0] < T_TILES:
            one_add()
            if sp_next[0] < T_TILES:
                second_product(sp_next[0], False)
                sp_next[0] += 1
            if sq_next[0] < T_TILES - 1:
                one_square()
        while sq_next[0] < T_TILES - 1:
            one_square()

        for q in range(SUB):
            transpose_back(q)

        stat = keep.tile([P, 2], F32)
        nc.vector.tensor_reduce(out=stat[:, 0:1], in_=sums[:, 0 : T_TILES - 1, 0], axis=AXIS_X, op=ALU.add)
        mean = ring_bank([P, 1], "mean")
        nc.tensor.matmul(out=mean[:], lhsT=averager[:], rhs=stat[:, 0:1], start=True, stop=False)
        nc.tensor.matmul(out=mean[:], lhsT=averager[:], rhs=sums[:, T_TILES - 1, 0:1], start=False, stop=True)
        square_last()
        nc.vector.tensor_reduce(out=stat[:, 1:2], in_=sums[:, 0 : T_TILES - 1, 1], axis=AXIS_X, op=ALU.add)
        mean_square = ring_bank([P, 1], "mean_square")
        nc.tensor.matmul(out=mean_square[:], lhsT=averager[:], rhs=stat[:, 1:2], start=True, stop=False)
        nc.tensor.matmul(out=mean_square[:], lhsT=averager[:], rhs=last_squares[:, 1:2], start=False, stop=False)
        nc.tensor.matmul(out=mean_square[:], lhsT=averager[:], rhs=last_squares[:, 0:1], start=False, stop=True)
        minus_mean = keep.tile([P, 1], F32)
        nc.vector.tensor_scalar(out=minus_mean[:], in0=mean[:], scalar1=-1.0, scalar2=None, op0=ALU.mult)
        eps_minus = keep.tile([P, 1], F32)
        nc.vector.tensor_scalar(
            out=eps_minus[:], in0=mean[:], scalar1=minus_mean[:], scalar2=EPS, op0=ALU.mult, op1=ALU.add
        )
        for q in range(SUB, PREFILL):
            transpose_back(q)
        rstd = keep.tile([P, 1], F32)
        nc.scalar.activation(out=rstd[:], in_=mean_square[:], func=ACT.Abs_reciprocal_sqrt, bias=eps_minus[:])
        shift = keep.tile([P, 1], F32)
        nc.scalar.activation(out=shift[:], in_=minus_mean[:], func=ACT.Identity, scale=rstd[:])

        def scale(q, halves):
            n, s = divmod(q, SUB)
            src = back_banks[q][:].rearrange("r (u e) m -> r u m e", e=2)[:, halves]
            dst = t_cols[:, n, s, :].rearrange("r (u m e) -> r u m e", u=2, e=2)[:, halves]
            if s % 2 == 0:
                nc.scalar.activation(out=dst, in_=src, func=ACT.Identity, scale=rstd[:], bias=shift[:])
            else:
                nc.vector.tensor_scalar(
                    out=dst, in0=src, scalar1=minus_mean[:], scalar2=rstd[:], op0=ALU.add, op1=ALU.mult
                )

        def store(n, first, last):
            rows = t_cols[:, n, :, :].rearrange("r s d -> r (s d)")
            nc.sync.dma_start(out=out_blocks[n][:, first:last], in_=rows[:, first:last])

        for q in range(N_PIECES):
            n, s = divmod(q, SUB)
            if q < 2:
                for u in range(2):
                    scale(q, slice(u, u + 1))
            else:
                scale(q, slice(0, 2))
            if q == 1:
                for u in range(2):
                    for r in (1, 0):
                        store(0, r * D + u * (D // 2), r * D + (u + 1) * (D // 2))
            elif s % 2 == 1 and n in (0, 1, N_BLOCKS - 1):
                store(n, (s - 1) * D, (s + 1) * D)
            elif s == SUB - 1:
                store(n, 0, SUB * D)
            if q + PREFILL < N_PIECES:
                transpose_back(q + PREFILL)
